import numpy as np
import ml_dtypes


def mxq(x, axis, fmt="e4m3"):
    dtype, down = {"e4m3": (ml_dtypes.float8_e4m3fn, 7), "e5m2": (ml_dtypes.float8_e5m2, 14)}[fmt]
    v = np.moveaxis(np.asarray(x, np.float32).astype(ml_dtypes.bfloat16).astype(np.float64), axis, -1)
    blocks = v.reshape(v.shape[:-1] + (-1, 32))
    amax = np.abs(blocks).max(-1, keepdims=True)
    byte = np.maximum(np.where(amax > 0, np.frexp(amax)[1] - 1 + 127, 0) - down, 1)
    scale = np.exp2(byte - 127.0)
    codes = (blocks / scale).astype(np.float32).astype(dtype).astype(np.float64)
    return np.moveaxis((codes * scale).reshape(v.shape), -1, axis)


WIDE = False


def mx_kscale(k):
    if not WIDE:
        return np.ones(k)
    levels = np.array([10, -10, 5, -5, 0])
    a = np.random.permutation(np.resize(levels, k // 512 * 4)).reshape(k // 512, 4)
    idx = np.arange(k)
    return np.exp2(a[idx // 512, idx % 128 // 32])


BF16 = ml_dtypes.bfloat16


def bf(x):
    return np.asarray(x, np.float32).astype(BF16)


def f64(x):
    return np.asarray(x).astype(np.float64)


B, T, H, HK, D, C = 1, 512, 16, 2, 128, 2048
G = H // HK
CLIP = 100.0
QS, KN, KB, VB = 9.0, 0.2, 9.0, 0.4


def setup_inputs():
    s = mx_kscale(C)
    kb = np.random.standard_normal(HK * D) * KB
    return {"x": bf(np.random.standard_normal((B, T, C)) * s),
            "Wv": bf(np.random.standard_normal((C, HK * D)) / np.sqrt(C) / s[:, None]),
            "bv": bf(np.random.standard_normal(HK * D) * VB),
            "q": bf(np.random.standard_normal((B, T, H * D)) * QS),
            "k": bf(np.random.standard_normal((B, T, HK * D)) * KN + kb)}


def reference(x, Wv, bv, q, k):
    v = (mxq(f64(x).reshape(B * T, C), 1, "e4m3") @ mxq(f64(Wv), 0, "e4m3")) + f64(bv)
    vh = v.reshape(B, T, HK, D).transpose(0, 2, 1, 3)
    qh = f64(q).reshape(B, T, HK, G, D).transpose(0, 2, 3, 1, 4).reshape(B, HK, G * T, D)
    kh = f64(k).reshape(B, T, HK, D).transpose(0, 2, 3, 1)
    s = np.clip(qh @ kh * (1.0 / np.sqrt(D)), -CLIP, CLIP)
    e = np.exp(s - s.max(-1, keepdims=True))
    o = (mxq(e, 3, "e4m3") @ mxq(vh, 2, "e4m3")) / e.sum(-1, keepdims=True)
    return o.reshape(B, HK, G, T, D).transpose(0, 3, 1, 2, 4).reshape(B, T, H * D)

@@ -1,0 +1,233 @@
+from contextlib import ExitStack
+import math
+
+import concourse.mybir as mybir
+from concourse.masks import make_identity
+
+F32 = mybir.dt.float32
+BF16 = mybir.dt.bfloat16
+U32 = mybir.dt.uint32
+U8 = mybir.dt.uint8
+FP8X4 = mybir.dt.float8_e4m3fn_x4
+ALU = mybir.AluOpType
+ACT = mybir.ActivationFunctionType
+
+P = 128
+PACK = 4
+K_PASS = P * PACK
+
+T = 512
+C = 2048
+H = 16
+HK = 2
+D = 128
+ROW_TILES = T // P
+PASSES = C // K_PASS
+HEADS_PER_GROUP = 4
+GROUPS = H // HEADS_PER_GROUP
+
+SCALE = 1.0 / math.sqrt(D)
+CLIP = 100.0
+RAW_CLIP = CLIP / SCALE
+
+FLOPS = 2 * T * C * HK * D + 2 * 2 * H * T * T * D
+
+
+def tile_multiqueryattention_pa_kernel(tc, x, Wv, bv, q, k, out):
+    nc = tc.nc
+    with ExitStack() as ctx:
+        keep = ctx.enter_context(tc.tile_pool(name="keep", bufs=1))
+        q_pool = ctx.enter_context(tc.tile_pool(name="q_pool", bufs=ROW_TILES))
+        qT_pool = ctx.enter_context(tc.tile_pool(name="qT_pool", bufs=2))
+        score_pool = ctx.enter_context(tc.tile_pool(name="score_pool", bufs=8))
+        work = ctx.enter_context(tc.tile_pool(name="work", bufs=3))
+        stats = ctx.enter_context(tc.tile_pool(name="stats", bufs=4))
+        psum_scores = ctx.enter_context(tc.psum_pool(name="psum_scores", bufs=3))
+        psum_turned = ctx.enter_context(tc.psum_pool(name="psum_turned", bufs=3))
+        psum_sums = ctx.enter_context(tc.psum_pool(name="psum_sums", bufs=2))
+
+        ident_f32 = keep.tile([P, P], F32)
+        make_identity(nc, ident_f32[:])
+        ident_bf16 = keep.tile([P, P], BF16)
+        make_identity(nc, ident_bf16[:])
+
+        x_view = x.flatten_outer_dims().rearrange("(r i) c -> r i c", i=ROW_TILES)
+        q_view = q.flatten_outer_dims().rearrange("(r i) c -> r i c", i=ROW_TILES)
+        k_view = k.flatten_outer_dims().rearrange("(r i) c -> r i c", i=ROW_TILES)
+        out_view = out.flatten_outer_dims().rearrange("(r i) c -> r i c", i=ROW_TILES)
+
+        k_rows = keep.tile([P, ROW_TILES, HK * D], BF16)
+        nc.sync.dma_start(out=k_rows[:], in_=k_view)
+        q_rows = []
+        for i in range(ROW_TILES):
+            q_rows.append(q_pool.tile([P, H * D], BF16, name="q_rows"))
+        nc.sync.dma_start(out=q_rows[0][:], in_=q_view[:, 0, :])
+        w_rows = keep.tile([P, C * HK * D // P], BF16)
+        nc.sync.dma_start(
+            out=w_rows[:].rearrange("p (s f) -> p s f", s=2 * PASSES),
+            in_=Wv.rearrange("(s p e) c -> p s (e c)", p=P, e=2),
+        )
+        x_rows = keep.tile([P, ROW_TILES, C], BF16)
+        for half in range(2):
+            cols = slice(half * C // 2, (half + 1) * C // 2)
+            nc.sync.dma_start(out=x_rows[:, :, cols], in_=x_view[:, :, cols])
+        bias_rows = keep.tile([P, HK * D], BF16)
+        nc.sync.dma_start(out=bias_rows[:], in_=bv.partition_broadcast(P))
+        for i in range(1, ROW_TILES):
+            nc.sync.dma_start(out=q_rows[i][:], in_=q_view[:, i, :])
+
+        def pack_rows_for_mx(blocks, codes, scales):
+            grouped = work.tile([P, 4 * K_PASS], BF16, align_bytes=64)
+            grouped_words = grouped[:].bitcast(F32).rearrange("p (b r u) -> p b r u", b=4, u=2)
+            for half in range(2):
+                turned = psum_turned.tile([P, 2, 2, P], F32, tag="turned")
+                for b in range(2):
+                    words = blocks[2 * half + b].bitcast(F32)
+                    for u in range(2):
+                        nc.tensor.transpose(turned[:, b, u, :], words[:, u * P : (u + 1) * P], ident_f32[:])
+                nc.scalar.copy(
+                    out=grouped_words[:, 2 * half : 2 * half + 2, :, :],
+                    in_=turned[:].rearrange("p b u r -> p b r u"),
+                )
+            nc.vector.quantize_mx(out=codes.bitcast(FP8X4), scales=scales, in_=grouped[:])
+
+        kT = keep.tile([P, HK, T], BF16)
+        k_turned = psum_turned.tile([P, HK, ROW_TILES, P], BF16, tag="turned")
+        for j in range(HK):
+            for i in range(ROW_TILES):
+                nc.tensor.transpose(k_turned[:, j, i, :], k_rows[:, i, j * D : (j + 1) * D], ident_bf16[:])
+        nc.scalar.copy(
+            out=kT[:].rearrange("p j (u r e) -> p j u r e", u=2, e=2),
+            in_=k_turned[:].rearrange("p j (u e) r -> p j u r e", u=2),
+        )
+
+        def turn_queries(i):
+            qT = qT_pool.tile([P, H, P], BF16)
+            for half in range(2):
+                q_turned = psum_turned.tile([P, H // 2, P], BF16, tag="turned")
+                for a in range(H // 2):
+                    h = half * (H // 2) + a
+                    nc.tensor.transpose(q_turned[:, a, :], q_rows[i][:, h * D : (h + 1) * D], ident_bf16[:])
+                nc.scalar.copy(out=qT[:, half * (H // 2) : (half + 1) * (H // 2), :], in_=q_turned[:])
+            return qT
+
+        qT_now = turn_queries(0)
+
+        x_codes = keep.tile([P, PASSES, T], U32, align_bytes=64)
+        x_scales = keep.tile([P, PASSES, T], U8, align_bytes=64)
+        for g in range(PASSES):
+            blocks = [x_rows[:, i, g * K_PASS : (g + 1) * K_PASS] for i in range(ROW_TILES)]
+            pack_rows_for_mx(blocks, x_codes[:, g, :], x_scales[:, g, :])
+
+        w_grouped = keep.tile([P, PASSES * HK * D * PACK], BF16, align_bytes=64)
+        w_codes = keep.tile([P, PASSES, HK * D], U32, align_bytes=64)
+        w_scales = keep.tile([P, PASSES, HK * D], U8, align_bytes=64)
+        per_pass = HK * D * PACK
+        for g in range(PASSES):
+            nc.vector.tensor_copy(
+                out=w_grouped[:, g * per_pass : (g + 1) * per_pass].rearrange("p (c t) -> p c t", t=PACK),
+                in_=w_rows[:, g * per_pass : (g + 1) * per_pass].rearrange("p (t c) -> p c t", t=PACK),
+            )
+        nc.vector.quantize_mx(
+            out=w_codes[:].rearrange("p g c -> p (g c)").bitcast(FP8X4),
+            scales=w_scales[:].rearrange("p g c -> p (g c)"),
+            in_=w_grouped[:],
+        )
+
+        v_grouped = keep.tile([P, HK, D, PACK], BF16, align_bytes=64)
+        for j in range(HK):
+            v_sums = psum_sums.tile([P, ROW_TILES, D], F32, tag="sums")
+            for i in range(ROW_TILES):
+                for g in range(PASSES):
+                    nc.tensor.matmul_mx(
+                        out=v_sums[:, i, :],
+                        lhsT=x_codes[:, g, i * P : (i + 1) * P].bitcast(FP8X4),
+                        lhsT_scale=x_scales[:, g, i * P : (i + 1) * P],
+                        rhs=w_codes[:, g, j * D : (j + 1) * D].bitcast(FP8X4),
+                        rhs_scale=w_scales[:, g, j * D : (j + 1) * D],
+                        start=(g == 0),
+                        stop=(g == PASSES - 1),
+                    )
+            nc.vector.tensor_tensor(
+                out=v_grouped[:, j, :, :],
+                in0=v_sums[:].rearrange("p t c -> p c t"),
+                in1=bias_rows[:, j * D : (j + 1) * D].unsqueeze(2).to_broadcast([P, D, PACK]),
+                op=ALU.add,
+            )
+        v_codes = keep.tile([P, HK * D], U32, align_bytes=64)
+        v_scales = keep.tile([P, HK * D], U8, align_bytes=64)
+        nc.vector.quantize_mx(
+            out=v_codes[:].bitcast(FP8X4),
+            scales=v_scales[:],
+            in_=v_grouped[:].rearrange("p j c t -> p (j c t)"),
+        )
+
+        for i in range(ROW_TILES):
+            qT = qT_now
+            for hq in range(GROUPS):
+                j = hq * HEADS_PER_GROUP * HK // H
+                row_max = stats.tile([P, HEADS_PER_GROUP], F32)
+                neg_max = stats.tile([P, HEADS_PER_GROUP], F32)
+                row_sum = stats.tile([P, HEADS_PER_GROUP], F32)
+                e_rows = work.tile([P, HEADS_PER_GROUP, T], BF16)
+                clipped = []
+                for a in range(HEADS_PER_GROUP):
+                    s_raw = psum_scores.tile([P, T], F32)
+                    nc.tensor.matmul(
+                        out=s_raw[:], lhsT=qT[:, hq * HEADS_PER_GROUP + a, :], rhs=kT[:, j, :], start=True, stop=True
+                    )
+                    s_clip = score_pool.tile([P, T], F32)
+                    nc.vector.tensor_scalar(
+                        out=s_clip[:],
+                        in0=s_raw[:],
+                        scalar1=RAW_CLIP,
+                        scalar2=-RAW_CLIP,
+                        op0=ALU.min,
+                        op1=ALU.max,
+                        accum_out=row_max[:, a : a + 1],
+                    )
+                    nc.gpsimd.tensor_scalar(
+                        out=s_clip[:], in0=s_clip[:], scalar1=RAW_CLIP, scalar2=-RAW_CLIP, op0=ALU.min, op1=ALU.max
+                    )
+                    clipped.append(s_clip)
+                nc.gpsimd.tensor_scalar(
+                    out=neg_max[:], in0=row_max[:], scalar1=-SCALE, scalar2=0.0, op0=ALU.mult, op1=ALU.add
+                )
+                for a in range(HEADS_PER_GROUP):
+                    nc.scalar.activation(
+                        out=e_rows[:, a, :],
+                        in_=clipped[a][:],
+                        func=ACT.Exp,
+                        bias=neg_max[:, a : a + 1],
+                        scale=SCALE,
+                        accum_out=row_sum[:, a : a + 1],
+                    )
+                if hq == 0 and i + 1 < ROW_TILES:
+                    qT_now = turn_queries(i + 1)
+
+                e_codes = work.tile([P, HEADS_PER_GROUP * P], U32, align_bytes=64)
+                e_scales = work.tile([P, HEADS_PER_GROUP * P], U8, align_bytes=64)
+                pack_rows_for_mx([e_rows[:, a, :] for a in range(HEADS_PER_GROUP)], e_codes[:], e_scales[:])
+
+                o_sums = psum_sums.tile([P, HEADS_PER_GROUP, D], F32, tag="sums")
+                for a in range(HEADS_PER_GROUP):
+                    nc.tensor.matmul_mx(
+                        out=o_sums[:, a, :],
+                        lhsT=e_codes[:, a * P : (a + 1) * P].bitcast(FP8X4),
+                        lhsT_scale=e_scales[:, a * P : (a + 1) * P],
+                        rhs=v_codes[:, j * D : (j + 1) * D].bitcast(FP8X4),
+                        rhs_scale=v_scales[:, j * D : (j + 1) * D],
+                        start=True,
+                        stop=True,
+                    )
+                inv_sum = stats.tile([P, HEADS_PER_GROUP], F32)
+                nc.vector.reciprocal(out=inv_sum[:], in_=row_sum[:])
+                o_rows = work.tile([P, HEADS_PER_GROUP, D], F32)
+                nc.vector.tensor_tensor(
+                    out=o_rows[:],
+                    in0=o_sums[:],
+                    in1=inv_sum[:].unsqueeze(2).to_broadcast([P, HEADS_PER_GROUP, D]),
+                    op=ALU.mult,
+                )
+                cols = slice(hq * HEADS_PER_GROUP * D, (hq + 1) * HEADS_PER_GROUP * D)
+                nc.sync.dma_start(out=out_view[:, i, cols], in_=o_rows[:].rearrange("p a d -> p (a d)"))

@@ -36,14 +36,15 @@ FLOPS = 2 * T * C * HK * D + 2 * 2 * H * T * T * D
 def tile_multiqueryattention_pa_kernel(tc, x, Wv, bv, q, k, out):
     nc = tc.nc
     with ExitStack() as ctx:
+        ctx.enter_context(tc.manual_schedule())
         keep = ctx.enter_context(tc.tile_pool(name="keep", bufs=1))
         q_pool = ctx.enter_context(tc.tile_pool(name="q_pool", bufs=ROW_TILES))
         qT_pool = ctx.enter_context(tc.tile_pool(name="qT_pool", bufs=2))
-        score_pool = ctx.enter_context(tc.tile_pool(name="score_pool", bufs=8))
+        score_pool = ctx.enter_context(tc.tile_pool(name="score_pool", bufs=2 * HEADS_PER_GROUP))
         work = ctx.enter_context(tc.tile_pool(name="work", bufs=3))
-        stats = ctx.enter_context(tc.tile_pool(name="stats", bufs=4))
-        psum_scores = ctx.enter_context(tc.psum_pool(name="psum_scores", bufs=3))
-        psum_turned = ctx.enter_context(tc.psum_pool(name="psum_turned", bufs=3))
+        stats = ctx.enter_context(tc.tile_pool(name="stats", bufs=6))
+        psum_scores = ctx.enter_context(tc.psum_pool(name="psum_scores", bufs=HEADS_PER_GROUP))
+        psum_turned = ctx.enter_context(tc.psum_pool(name="psum_turned", bufs=2))
         psum_sums = ctx.enter_context(tc.psum_pool(name="psum_sums", bufs=2))
 
         ident_f32 = keep.tile([P, P], F32)
@@ -56,12 +57,6 @@ def tile_multiqueryattention_pa_kernel(tc, x, Wv, bv, q, k, out):
         k_view = k.flatten_outer_dims().rearrange("(r i) c -> r i c", i=ROW_TILES)
         out_view = out.flatten_outer_dims().rearrange("(r i) c -> r i c", i=ROW_TILES)
 
-        k_rows = keep.tile([P, ROW_TILES, HK * D], BF16)
-        nc.sync.dma_start(out=k_rows[:], in_=k_view)
-        q_rows = []
-        for i in range(ROW_TILES):
-            q_rows.append(q_pool.tile([P, H * D], BF16, name="q_rows"))
-        nc.sync.dma_start(out=q_rows[0][:], in_=q_view[:, 0, :])
         w_rows = keep.tile([P, C * HK * D // P], BF16)
         nc.sync.dma_start(
             out=w_rows[:].rearrange("p (s f) -> p s f", s=2 * PASSES),
@@ -71,12 +66,18 @@ def tile_multiqueryattention_pa_kernel(tc, x, Wv, bv, q, k, out):
         for half in range(2):
             cols = slice(half * C // 2, (half + 1) * C // 2)
             nc.sync.dma_start(out=x_rows[:, :, cols], in_=x_view[:, :, cols])
+        k_rows = keep.tile([P, ROW_TILES, HK * D], BF16)
+        nc.sync.dma_start(out=k_rows[:], in_=k_view)
+        q_rows = []
+        for i in range(ROW_TILES):
+            q_rows.append(q_pool.tile([P, H * D], BF16, name="q_rows"))
+        nc.sync.dma_start(out=q_rows[0][:], in_=q_view[:, 0, :])
         bias_rows = keep.tile([P, HK * D], BF16)
         nc.sync.dma_start(out=bias_rows[:], in_=bv.partition_broadcast(P))
         for i in range(1, ROW_TILES):
             nc.sync.dma_start(out=q_rows[i][:], in_=q_view[:, i, :])
 
-        def pack_rows_for_mx(blocks, codes, scales):
+        def turn_blocks(blocks):
             grouped = work.tile([P, 4 * K_PASS], BF16, align_bytes=64)
             grouped_words = grouped[:].bitcast(F32).rearrange("p (b r u) -> p b r u", b=4, u=2)
             for half in range(2):
@@ -89,35 +90,7 @@ def tile_multiqueryattention_pa_kernel(tc, x, Wv, bv, q, k, out):
                     out=grouped_words[:, 2 * half : 2 * half + 2, :, :],
                     in_=turned[:].rearrange("p b u r -> p b r u"),
                 )
-            nc.vector.quantize_mx(out=codes.bitcast(FP8X4), scales=scales, in_=grouped[:])
-
-        kT = keep.tile([P, HK, T], BF16)
-        k_turned = psum_turned.tile([P, HK, ROW_TILES, P], BF16, tag="turned")
-        for j in range(HK):
-            for i in range(ROW_TILES):
-                nc.tensor.transpose(k_turned[:, j, i, :], k_rows[:, i, j * D : (j + 1) * D], ident_bf16[:])
-        nc.scalar.copy(
-            out=kT[:].rearrange("p j (u r e) -> p j u r e", u=2, e=2),
-            in_=k_turned[:].rearrange("p j (u e) r -> p j u r e", u=2),
-        )
-
-        def turn_queries(i):
-            qT = qT_pool.tile([P, H, P], BF16)
-            for half in range(2):
-                q_turned = psum_turned.tile([P, H // 2, P], BF16, tag="turned")
-                for a in range(H // 2):
-                    h = half * (H // 2) + a
-                    nc.tensor.transpose(q_turned[:, a, :], q_rows[i][:, h * D : (h + 1) * D], ident_bf16[:])
-                nc.scalar.copy(out=qT[:, half * (H // 2) : (half + 1) * (H // 2), :], in_=q_turned[:])
-            return qT
-
-        qT_now = turn_queries(0)
-
-        x_codes = keep.tile([P, PASSES, T], U32, align_bytes=64)
-        x_scales = keep.tile([P, PASSES, T], U8, align_bytes=64)
-        for g in range(PASSES):
-            blocks = [x_rows[:, i, g * K_PASS : (g + 1) * K_PASS] for i in range(ROW_TILES)]
-            pack_rows_for_mx(blocks, x_codes[:, g, :], x_scales[:, g, :])
+            return grouped
 
         w_grouped = keep.tile([P, PASSES * HK * D * PACK], BF16, align_bytes=64)
         w_codes = keep.tile([P, PASSES, HK * D], U32, align_bytes=64)
@@ -133,14 +106,143 @@ def tile_multiqueryattention_pa_kernel(tc, x, Wv, bv, q, k, out):
             scales=w_scales[:].rearrange("p g c -> p (g c)"),
             in_=w_grouped[:],
         )
+        x_codes = keep.tile([P, PASSES, T], U32, align_bytes=64)
+        x_scales = keep.tile([P, PASSES, T], U8, align_bytes=64)
+        for g in range(PASSES):
+            x_grouped = turn_blocks([x_rows[:, i, g * K_PASS : (g + 1) * K_PASS] for i in range(ROW_TILES)])
+            nc.vector.quantize_mx(out=x_codes[:, g, :].bitcast(FP8X4), scales=x_scales[:, g, :], in_=x_grouped[:])
 
-        v_grouped = keep.tile([P, HK, D, PACK], BF16, align_bytes=64)
+        kT = keep.tile([P, HK, T], BF16)
+        k_turned = psum_turned.tile([P, HK, ROW_TILES, P], BF16, tag="turned")
         for j in range(HK):
-            v_sums = psum_sums.tile([P, ROW_TILES, D], F32, tag="sums")
+            for i in range(ROW_TILES):
+                nc.tensor.transpose(k_turned[:, j, i, :], k_rows[:, i, j * D : (j + 1) * D], ident_bf16[:])
+        nc.scalar.copy(
+            out=kT[:].rearrange("p j (u r e) -> p j u r e", u=2, e=2),
+            in_=k_turned[:].rearrange("p j (u e) r -> p j u r e", u=2),
+        )
+
+        qT = [None] * ROW_TILES
+
+        def turn_queries(i, half):
+            if half == 0:
+                qT[i] = qT_pool.tile([P, H, P], BF16, name="qT")
+            q_turned = psum_turned.tile([P, H // 2, P], BF16, tag="turned")
+            for a in range(H // 2):
+                h = half * (H // 2) + a
+                nc.tensor.transpose(q_turned[:, a, :], q_rows[i][:, h * D : (h + 1) * D], ident_bf16[:])
+            nc.scalar.copy(out=qT[i][:, half * (H // 2) : (half + 1) * (H // 2), :], in_=q_turned[:])
+
+        turn_queries(0, 0)
+        turn_queries(0, 1)
+
+        N = ROW_TILES * GROUPS
+        raw_scores = [None] * N
+        clipped = [None] * N
+        neg_max = [None] * N
+        row_sum = [None] * N
+        e_grouped = [None] * N
+        e_codes = [None] * N
+        e_scales = [None] * N
+        o_sums = [None] * N
+        v_codes = keep.tile([P, HK * D], U32, align_bytes=64)
+        v_scales = keep.tile([P, HK * D], U8, align_bytes=64)
+
+        def kv_head(n):
+            return (n % GROUPS) * HEADS_PER_GROUP * HK // H
+
+        def score_matmuls(n):
+            i, hq = divmod(n, GROUPS)
+            raw_scores[n] = []
+            for a in range(HEADS_PER_GROUP):
+                s_raw = psum_scores.tile([P, T], F32)
+                nc.tensor.matmul(
+                    out=s_raw[:],
+                    lhsT=qT[i][:, hq * HEADS_PER_GROUP + a, :],
+                    rhs=kT[:, kv_head(n), :],
+                    start=True,
+                    stop=True,
+                )
+                raw_scores[n].append(s_raw)
+
+        def clip_and_max(n):
+            row_max = stats.tile([P, HEADS_PER_GROUP], F32)
+            clipped[n] = []
+            for a in range(HEADS_PER_GROUP):
+                s_clip = score_pool.tile([P, T], F32)
+                nc.vector.tensor_scalar(
+                    out=s_clip[:],
+                    in0=raw_scores[n][a][:],
+                    scalar1=RAW_CLIP,
+                    scalar2=-RAW_CLIP,
+                    op0=ALU.min,
+                    op1=ALU.max,
+                    accum_out=row_max[:, a : a + 1],
+                )
+                nc.gpsimd.tensor_scalar(
+                    out=s_clip[:], in0=s_clip[:], scalar1=RAW_CLIP, scalar2=-RAW_CLIP, op0=ALU.min, op1=ALU.max
+                )
+                clipped[n].append(s_clip)
+            neg_max[n] = stats.tile([P, HEADS_PER_GROUP], F32, name="neg_max")
+            nc.gpsimd.tensor_scalar(
+                out=neg_max[n][:], in0=row_max[:], scalar1=-SCALE, scalar2=0.0, op0=ALU.mult, op1=ALU.add
+            )
+
+        def exp_and_turn(n):
+            row_sum[n] = stats.tile([P, HEADS_PER_GROUP], F32, name="row_sum")
+            e_rows = work.tile([P, HEADS_PER_GROUP, T], BF16)
+            for a in range(HEADS_PER_GROUP):
+                nc.scalar.activation(
+                    out=e_rows[:, a, :],
+                    in_=clipped[n][a][:],
+                    func=ACT.Exp,
+                    bias=neg_max[n][:, a : a + 1],
+                    scale=SCALE,
+                    accum_out=row_sum[n][:, a : a + 1],
+                )
+            e_grouped[n] = turn_blocks([e_rows[:, a, :] for a in range(HEADS_PER_GROUP)])
+
+        def quantise_e(n):
+            e_codes[n] = work.tile([P, HEADS_PER_GROUP * P], U32, align_bytes=64, name="e_codes")
+            e_scales[n] = work.tile([P, HEADS_PER_GROUP * P], U8, align_bytes=64, name="e_scales")
+            nc.vector.quantize_mx(out=e_codes[n][:].bitcast(FP8X4), scales=e_scales[n][:], in_=e_grouped[n][:])
+
+        def weighted_sums(n):
+            j = kv_head(n)
+            o_sums[n] = psum_sums.tile([P, HEADS_PER_GROUP, D], F32, tag="sums", name="o_sums")
+            for a in range(HEADS_PER_GROUP):
+                nc.tensor.matmul_mx(
+                    out=o_sums[n][:, a, :],
+                    lhsT=e_codes[n][:, a * P : (a + 1) * P].bitcast(FP8X4),
+                    lhsT_scale=e_scales[n][:, a * P : (a + 1) * P],
+                    rhs=v_codes[:, j * D : (j + 1) * D].bitcast(FP8X4),
+                    rhs_scale=v_scales[:, j * D : (j + 1) * D],
+                    start=True,
+                    stop=True,
+                )
+
+        def normalise_and_store(n):
+            i, hq = divmod(n, GROUPS)
+            inv_sum = stats.tile([P, HEADS_PER_GROUP], F32)
+            nc.vector.reciprocal(out=inv_sum[:], in_=row_sum[n][:])
+            o_rows = work.tile([P, HEADS_PER_GROUP, D], F32)
+            nc.vector.tensor_tensor(
+                out=o_rows[:],
+                in0=o_sums[n][:],
+                in1=inv_sum[:].unsqueeze(2).to_broadcast([P, HEADS_PER_GROUP, D]),
+                op=ALU.mult,
+            )
+            cols = slice(hq * HEADS_PER_GROUP * D, (hq + 1) * HEADS_PER_GROUP * D)
+            nc.sync.dma_start(out=out_view[:, i, cols], in_=o_rows[:].rearrange("p a d -> p (a d)"))
+
+        score_matmuls(0)
+        v_sums = []
+        for j in range(HK):
+            v_sums.append(psum_sums.tile([P, ROW_TILES, D], F32, tag="sums", name="v_sums"))
             for i in range(ROW_TILES):
                 for g in range(PASSES):
                     nc.tensor.matmul_mx(
-                        out=v_sums[:, i, :],
+                        out=v_sums[j][:, i, :],
                         lhsT=x_codes[:, g, i * P : (i + 1) * P].bitcast(FP8X4),
                         lhsT_scale=x_scales[:, g, i * P : (i + 1) * P],
                         rhs=w_codes[:, g, j * D : (j + 1) * D].bitcast(FP8X4),
@@ -148,86 +250,34 @@ def tile_multiqueryattention_pa_kernel(tc, x, Wv, bv, q, k, out):
                         start=(g == 0),
                         stop=(g == PASSES - 1),
                     )
+        clip_and_max(0)
+        score_matmuls(1)
+        v_grouped = keep.tile([P, HK, D, PACK], BF16, align_bytes=64)
+        for j in range(HK):
             nc.vector.tensor_tensor(
                 out=v_grouped[:, j, :, :],
-                in0=v_sums[:].rearrange("p t c -> p c t"),
+                in0=v_sums[j][:].rearrange("p t c -> p c t"),
                 in1=bias_rows[:, j * D : (j + 1) * D].unsqueeze(2).to_broadcast([P, D, PACK]),
                 op=ALU.add,
             )
-        v_codes = keep.tile([P, HK * D], U32, align_bytes=64)
-        v_scales = keep.tile([P, HK * D], U8, align_bytes=64)
         nc.vector.quantize_mx(
             out=v_codes[:].bitcast(FP8X4),
             scales=v_scales[:],
             in_=v_grouped[:].rearrange("p j c t -> p (j c t)"),
         )
 
-        for i in range(ROW_TILES):
-            qT = qT_now
-            for hq in range(GROUPS):
-                j = hq * HEADS_PER_GROUP * HK // H
-                row_max = stats.tile([P, HEADS_PER_GROUP], F32)
-                neg_max = stats.tile([P, HEADS_PER_GROUP], F32)
-                row_sum = stats.tile([P, HEADS_PER_GROUP], F32)
-                e_rows = work.tile([P, HEADS_PER_GROUP, T], BF16)
-                clipped = []
-                for a in range(HEADS_PER_GROUP):
-                    s_raw = psum_scores.tile([P, T], F32)
-                    nc.tensor.matmul(
-                        out=s_raw[:], lhsT=qT[:, hq * HEADS_PER_GROUP + a, :], rhs=kT[:, j, :], start=True, stop=True
-                    )
-                    s_clip = score_pool.tile([P, T], F32)
-                    nc.vector.tensor_scalar(
-                        out=s_clip[:],
-                        in0=s_raw[:],
-                        scalar1=RAW_CLIP,
-                        scalar2=-RAW_CLIP,
-                        op0=ALU.min,
-                        op1=ALU.max,
-                        accum_out=row_max[:, a : a + 1],
-                    )
-                    nc.gpsimd.tensor_scalar(
-                        out=s_clip[:], in0=s_clip[:], scalar1=RAW_CLIP, scalar2=-RAW_CLIP, op0=ALU.min, op1=ALU.max
-                    )
-                    clipped.append(s_clip)
-                nc.gpsimd.tensor_scalar(
-                    out=neg_max[:], in0=row_max[:], scalar1=-SCALE, scalar2=0.0, op0=ALU.mult, op1=ALU.add
-                )
-                for a in range(HEADS_PER_GROUP):
-                    nc.scalar.activation(
-                        out=e_rows[:, a, :],
-                        in_=clipped[a][:],
-                        func=ACT.Exp,
-                        bias=neg_max[:, a : a + 1],
-                        scale=SCALE,
-                        accum_out=row_sum[:, a : a + 1],
-                    )
-                if hq == 0 and i + 1 < ROW_TILES:
-                    qT_now = turn_queries(i + 1)
-
-                e_codes = work.tile([P, HEADS_PER_GROUP * P], U32, align_bytes=64)
-                e_scales = work.tile([P, HEADS_PER_GROUP * P], U8, align_bytes=64)
-                pack_rows_for_mx([e_rows[:, a, :] for a in range(HEADS_PER_GROUP)], e_codes[:], e_scales[:])
-
-                o_sums = psum_sums.tile([P, HEADS_PER_GROUP, D], F32, tag="sums")
-                for a in range(HEADS_PER_GROUP):
-                    nc.tensor.matmul_mx(
-                        out=o_sums[:, a, :],
-                        lhsT=e_codes[:, a * P : (a + 1) * P].bitcast(FP8X4),
-                        lhsT_scale=e_scales[:, a * P : (a + 1) * P],
-                        rhs=v_codes[:, j * D : (j + 1) * D].bitcast(FP8X4),
-                        rhs_scale=v_scales[:, j * D : (j + 1) * D],
-                        start=True,
-                        stop=True,
-                    )
-                inv_sum = stats.tile([P, HEADS_PER_GROUP], F32)
-                nc.vector.reciprocal(out=inv_sum[:], in_=row_sum[:])
-                o_rows = work.tile([P, HEADS_PER_GROUP, D], F32)
-                nc.vector.tensor_tensor(
-                    out=o_rows[:],
-                    in0=o_sums[:],
-                    in1=inv_sum[:].unsqueeze(2).to_broadcast([P, HEADS_PER_GROUP, D]),
-                    op=ALU.mult,
-                )
-                cols = slice(hq * HEADS_PER_GROUP * D, (hq + 1) * HEADS_PER_GROUP * D)
-                nc.sync.dma_start(out=out_view[:, i, cols], in_=o_rows[:].rearrange("p a d -> p (a d)"))
+        for n in range(1, N + 5):
+            if 0 <= n - 4 < N:
+                normalise_and_store(n - 4)
+            if n < N:
+                clip_and_max(n)
+            if 0 <= n - 2 < N:
+                quantise_e(n - 2)
+            if 0 <= n - 3 < N:
+                weighted_sums(n - 3)
+            if n - 1 < N:
+                exp_and_turn(n - 1)
+            if n // GROUPS + 1 < ROW_TILES and n % GROUPS in (1, 2):
+                turn_queries(n // GROUPS + 1, n % GROUPS - 1)
+            if n + 1 < N:
+                score_matmuls(n + 1)

@@ -24,6 +24,7 @@ D = 128
 ROW_TILES = T // P
 PASSES = C // K_PASS
 HEADS_PER_GROUP = 4
+GPSIMD_CLIPS = 2
 GROUPS = H // HEADS_PER_GROUP
 
 SCALE = 1.0 / math.sqrt(D)
@@ -41,6 +42,7 @@ def tile_multiqueryattention_pa_kernel(tc, x, Wv, bv, q, k, out):
         q_pool = ctx.enter_context(tc.tile_pool(name="q_pool", bufs=ROW_TILES))
         qT_pool = ctx.enter_context(tc.tile_pool(name="qT_pool", bufs=2))
         score_pool = ctx.enter_context(tc.tile_pool(name="score_pool", bufs=2 * HEADS_PER_GROUP))
+        x_pool = ctx.enter_context(tc.tile_pool(name="x_pool", bufs=PASSES))
         work = ctx.enter_context(tc.tile_pool(name="work", bufs=3))
         stats = ctx.enter_context(tc.tile_pool(name="stats", bufs=6))
         psum_scores = ctx.enter_context(tc.psum_pool(name="psum_scores", bufs=HEADS_PER_GROUP))
@@ -62,24 +64,23 @@ def tile_multiqueryattention_pa_kernel(tc, x, Wv, bv, q, k, out):
             out=w_rows[:].rearrange("p (s f) -> p s f", s=2 * PASSES),
             in_=Wv.rearrange("(s p e) c -> p s (e c)", p=P, e=2),
         )
-        x_rows = keep.tile([P, ROW_TILES, C], BF16)
-        for half in range(2):
-            cols = slice(half * C // 2, (half + 1) * C // 2)
-            nc.sync.dma_start(out=x_rows[:, :, cols], in_=x_view[:, :, cols])
         k_rows = keep.tile([P, ROW_TILES, HK * D], BF16)
         nc.sync.dma_start(out=k_rows[:], in_=k_view)
         q_rows = []
         for i in range(ROW_TILES):
             q_rows.append(q_pool.tile([P, H * D], BF16, name="q_rows"))
         nc.sync.dma_start(out=q_rows[0][:], in_=q_view[:, 0, :])
+        x_rows = keep.tile([P, ROW_TILES, C], BF16)
+        for half in range(2):
+            cols = slice(half * C // 2, (half + 1) * C // 2)
+            nc.sync.dma_start(out=x_rows[:, :, cols], in_=x_view[:, :, cols])
         bias_rows = keep.tile([P, HK * D], BF16)
         nc.sync.dma_start(out=bias_rows[:], in_=bv.partition_broadcast(P))
         for i in range(1, ROW_TILES):
             nc.sync.dma_start(out=q_rows[i][:], in_=q_view[:, i, :])
 
-        def turn_blocks(blocks):
-            grouped = work.tile([P, 4 * K_PASS], BF16, align_bytes=64)
-            grouped_words = grouped[:].bitcast(F32).rearrange("p (b r u) -> p b r u", b=4, u=2)
+        def turn_blocks(blocks, grouped):
+            grouped_words = grouped.bitcast(F32).rearrange("p (b r u) -> p b r u", b=4, u=2)
             for half in range(2):
                 turned = psum_turned.tile([P, 2, 2, P], F32, tag="turned")
                 for b in range(2):
@@ -90,7 +91,6 @@ def tile_multiqueryattention_pa_kernel(tc, x, Wv, bv, q, k, out):
                     out=grouped_words[:, 2 * half : 2 * half + 2, :, :],
                     in_=turned[:].rearrange("p b u r -> p b r u"),
                 )
-            return grouped
 
         w_grouped = keep.tile([P, PASSES * HK * D * PACK], BF16, align_bytes=64)
         w_codes = keep.tile([P, PASSES, HK * D], U32, align_bytes=64)
@@ -106,11 +106,6 @@ def tile_multiqueryattention_pa_kernel(tc, x, Wv, bv, q, k, out):
             scales=w_scales[:].rearrange("p g c -> p (g c)"),
             in_=w_grouped[:],
         )
-        x_codes = keep.tile([P, PASSES, T], U32, align_bytes=64)
-        x_scales = keep.tile([P, PASSES, T], U8, align_bytes=64)
-        for g in range(PASSES):
-            x_grouped = turn_blocks([x_rows[:, i, g * K_PASS : (g + 1) * K_PASS] for i in range(ROW_TILES)])
-            nc.vector.quantize_mx(out=x_codes[:, g, :].bitcast(FP8X4), scales=x_scales[:, g, :], in_=x_grouped[:])
 
         kT = keep.tile([P, HK, T], BF16)
         k_turned = psum_turned.tile([P, HK, ROW_TILES, P], BF16, tag="turned")
@@ -136,17 +131,60 @@ def tile_multiqueryattention_pa_kernel(tc, x, Wv, bv, q, k, out):
         turn_queries(0, 0)
         turn_queries(0, 1)
 
+        x_codes = keep.tile([P, PASSES, T], U32, align_bytes=64)
+        x_scales = keep.tile([P, PASSES, T], U8, align_bytes=64)
+        v_sums = []
+        v_codes = keep.tile([P, HK * D], U32, align_bytes=64)
+        v_scales = keep.tile([P, HK * D], U8, align_bytes=64)
+
+        def quantise_x():
+            for g in range(PASSES):
+                x_grouped = x_pool.tile([P, 4 * K_PASS], BF16, align_bytes=64)
+                turn_blocks([x_rows[:, i, g * K_PASS : (g + 1) * K_PASS] for i in range(ROW_TILES)], x_grouped[:])
+                nc.vector.quantize_mx(
+                    out=x_codes[:, g, :].bitcast(FP8X4), scales=x_scales[:, g, :], in_=x_grouped[:]
+                )
+
+        def value_matmuls():
+            for j in range(HK):
+                v_sums.append(psum_sums.tile([P, ROW_TILES, D], F32, tag="sums", name="v_sums"))
+                for i in range(ROW_TILES):
+                    for g in range(PASSES):
+                        nc.tensor.matmul_mx(
+                            out=v_sums[j][:, i, :],
+                            lhsT=x_codes[:, g, i * P : (i + 1) * P].bitcast(FP8X4),
+                            lhsT_scale=x_scales[:, g, i * P : (i + 1) * P],
+                            rhs=w_codes[:, g, j * D : (j + 1) * D].bitcast(FP8X4),
+                            rhs_scale=w_scales[:, g, j * D : (j + 1) * D],
+                            start=(g == 0),
+                            stop=(g == PASSES - 1),
+                        )
+
+        def quantise_v():
+            v_grouped = keep.tile([P, HK, D, PACK], BF16, align_bytes=64)
+            for j in range(HK):
+                nc.vector.tensor_tensor(
+                    out=v_grouped[:, j, :, :],
+                    in0=v_sums[j][:].rearrange("p t c -> p c t"),
+                    in1=bias_rows[:, j * D : (j + 1) * D].unsqueeze(2).to_broadcast([P, D, PACK]),
+                    op=ALU.add,
+                )
+            nc.vector.quantize_mx(
+                out=v_codes[:].bitcast(FP8X4),
+                scales=v_scales[:],
+                in_=v_grouped[:].rearrange("p j c t -> p (j c t)"),
+            )
+
         N = ROW_TILES * GROUPS
         raw_scores = [None] * N
         clipped = [None] * N
+        row_max = [None] * N
         neg_max = [None] * N
         row_sum = [None] * N
         e_grouped = [None] * N
         e_codes = [None] * N
         e_scales = [None] * N
         o_sums = [None] * N
-        v_codes = keep.tile([P, HK * D], U32, align_bytes=64)
-        v_scales = keep.tile([P, HK * D], U8, align_bytes=64)
 
         def kv_head(n):
             return (n % GROUPS) * HEADS_PER_GROUP * HK // H
@@ -165,8 +203,8 @@ def tile_multiqueryattention_pa_kernel(tc, x, Wv, bv, q, k, out):
                 )
                 raw_scores[n].append(s_raw)
 
-        def clip_and_max(n):
-            row_max = stats.tile([P, HEADS_PER_GROUP], F32)
+        def upper_clip_and_max(n):
+            row_max[n] = stats.tile([P, HEADS_PER_GROUP], F32, name="row_max")
             clipped[n] = []
             for a in range(HEADS_PER_GROUP):
                 s_clip = score_pool.tile([P, T], F32)
@@ -177,16 +215,24 @@ def tile_multiqueryattention_pa_kernel(tc, x, Wv, bv, q, k, out):
                     scalar2=-RAW_CLIP,
                     op0=ALU.min,
                     op1=ALU.max,
-                    accum_out=row_max[:, a : a + 1],
-                )
-                nc.gpsimd.tensor_scalar(
-                    out=s_clip[:], in0=s_clip[:], scalar1=RAW_CLIP, scalar2=-RAW_CLIP, op0=ALU.min, op1=ALU.max
+                    accum_out=row_max[n][:, a : a + 1],
                 )
                 clipped[n].append(s_clip)
+                if a < GPSIMD_CLIPS:
+                    nc.gpsimd.tensor_scalar(
+                        out=s_clip[:],
+                        in0=s_clip[:],
+                        scalar1=RAW_CLIP,
+                        scalar2=-RAW_CLIP,
+                        op0=ALU.min,
+                        op1=ALU.max,
+                    )
+
+        def lower_clip_on_vector(n):
             neg_max[n] = stats.tile([P, HEADS_PER_GROUP], F32, name="neg_max")
-            nc.gpsimd.tensor_scalar(
-                out=neg_max[n][:], in0=row_max[:], scalar1=-SCALE, scalar2=0.0, op0=ALU.mult, op1=ALU.add
-            )
+            nc.vector.tensor_scalar_mul(out=neg_max[n][:], in0=row_max[n][:], scalar1=-SCALE)
+            for a in range(GPSIMD_CLIPS, HEADS_PER_GROUP):
+                nc.vector.tensor_scalar_max(out=clipped[n][a][:], in0=clipped[n][a][:], scalar1=-RAW_CLIP)
 
         def exp_and_turn(n):
             row_sum[n] = stats.tile([P, HEADS_PER_GROUP], F32, name="row_sum")
@@ -200,7 +246,8 @@ def tile_multiqueryattention_pa_kernel(tc, x, Wv, bv, q, k, out):
                     scale=SCALE,
                     accum_out=row_sum[n][:, a : a + 1],
                 )
-            e_grouped[n] = turn_blocks([e_rows[:, a, :] for a in range(HEADS_PER_GROUP)])
+            e_grouped[n] = work.tile([P, 4 * K_PASS], BF16, align_bytes=64, name="e_grouped")
+            turn_blocks([e_rows[:, a, :] for a in range(HEADS_PER_GROUP)], e_grouped[n][:])
 
         def quantise_e(n):
             e_codes[n] = work.tile([P, HEADS_PER_GROUP * P], U32, align_bytes=64, name="e_codes")
@@ -236,47 +283,25 @@ def tile_multiqueryattention_pa_kernel(tc, x, Wv, bv, q, k, out):
             nc.sync.dma_start(out=out_view[:, i, cols], in_=o_rows[:].rearrange("p a d -> p (a d)"))
 
         score_matmuls(0)
-        v_sums = []
-        for j in range(HK):
-            v_sums.append(psum_sums.tile([P, ROW_TILES, D], F32, tag="sums", name="v_sums"))
-            for i in range(ROW_TILES):
-                for g in range(PASSES):
-                    nc.tensor.matmul_mx(
-                        out=v_sums[j][:, i, :],
-                        lhsT=x_codes[:, g, i * P : (i + 1) * P].bitcast(FP8X4),
-                        lhsT_scale=x_scales[:, g, i * P : (i + 1) * P],
-                        rhs=w_codes[:, g, j * D : (j + 1) * D].bitcast(FP8X4),
-                        rhs_scale=w_scales[:, g, j * D : (j + 1) * D],
-                        start=(g == 0),
-                        stop=(g == PASSES - 1),
-                    )
-        clip_and_max(0)
-        score_matmuls(1)
-        v_grouped = keep.tile([P, HK, D, PACK], BF16, align_bytes=64)
-        for j in range(HK):
-            nc.vector.tensor_tensor(
-                out=v_grouped[:, j, :, :],
-                in0=v_sums[j][:].rearrange("p t c -> p c t"),
-                in1=bias_rows[:, j * D : (j + 1) * D].unsqueeze(2).to_broadcast([P, D, PACK]),
-                op=ALU.add,
-            )
-        nc.vector.quantize_mx(
-            out=v_codes[:].bitcast(FP8X4),
-            scales=v_scales[:],
-            in_=v_grouped[:].rearrange("p j c t -> p (j c t)"),
-        )
-
-        for n in range(1, N + 5):
-            if 0 <= n - 4 < N:
+        for n in range(N + 4):
+            if n < N:
+                upper_clip_and_max(n)
+            if 0 <= n - 4:
                 normalise_and_store(n - 4)
             if n < N:
-                clip_and_max(n)
+                lower_clip_on_vector(n)
+            if n == 2:
+                quantise_v()
             if 0 <= n - 2 < N:
                 quantise_e(n - 2)
             if 0 <= n - 3 < N:
                 weighted_sums(n - 3)
-            if n - 1 < N:
+            if 0 <= n - 1 < N:
                 exp_and_turn(n - 1)
+            if n == 0:
+                quantise_x()
+            if n == 1:
+                value_matmuls()
             if n // GROUPS + 1 < ROW_TILES and n % GROUPS in (1, 2):
                 turn_queries(n // GROUPS + 1, n % GROUPS - 1)
             if n + 1 < N:

@@ -23,9 +23,9 @@ HK = 2
 D = 128
 ROW_TILES = T // P
 PASSES = C // K_PASS
-HEADS_PER_GROUP = 4
-GPSIMD_CLIPS = 2
-GROUPS = H // HEADS_PER_GROUP
+PAIR = 2
+GROUP = 4
+PAIRS_PER_TILE = H // PAIR
 
 SCALE = 1.0 / math.sqrt(D)
 CLIP = 100.0
@@ -41,268 +41,348 @@ def tile_multiqueryattention_pa_kernel(tc, x, Wv, bv, q, k, out):
         keep = ctx.enter_context(tc.tile_pool(name="keep", bufs=1))
         q_pool = ctx.enter_context(tc.tile_pool(name="q_pool", bufs=ROW_TILES))
         qT_pool = ctx.enter_context(tc.tile_pool(name="qT_pool", bufs=2))
-        score_pool = ctx.enter_context(tc.tile_pool(name="score_pool", bufs=2 * HEADS_PER_GROUP))
+        score_pool = ctx.enter_context(tc.tile_pool(name="score_pool", bufs=4 * PAIR))
         x_pool = ctx.enter_context(tc.tile_pool(name="x_pool", bufs=PASSES))
-        work = ctx.enter_context(tc.tile_pool(name="work", bufs=3))
-        stats = ctx.enter_context(tc.tile_pool(name="stats", bufs=6))
-        psum_scores = ctx.enter_context(tc.psum_pool(name="psum_scores", bufs=HEADS_PER_GROUP))
+        work = ctx.enter_context(tc.tile_pool(name="work", bufs=6))
+        stats = ctx.enter_context(tc.tile_pool(name="stats", bufs=16))
+        psum_scores = ctx.enter_context(tc.psum_pool(name="psum_scores", bufs=2 * PAIR))
         psum_turned = ctx.enter_context(tc.psum_pool(name="psum_turned", bufs=2))
         psum_sums = ctx.enter_context(tc.psum_pool(name="psum_sums", bufs=2))
-
-        ident_f32 = keep.tile([P, P], F32)
-        make_identity(nc, ident_f32[:])
-        ident_bf16 = keep.tile([P, P], BF16)
-        make_identity(nc, ident_bf16[:])
 
         x_view = x.flatten_outer_dims().rearrange("(r i) c -> r i c", i=ROW_TILES)
         q_view = q.flatten_outer_dims().rearrange("(r i) c -> r i c", i=ROW_TILES)
         k_view = k.flatten_outer_dims().rearrange("(r i) c -> r i c", i=ROW_TILES)
         out_view = out.flatten_outer_dims().rearrange("(r i) c -> r i c", i=ROW_TILES)
 
-        w_rows = keep.tile([P, C * HK * D // P], BF16)
-        nc.sync.dma_start(
-            out=w_rows[:].rearrange("p (s f) -> p s f", s=2 * PASSES),
-            in_=Wv.rearrange("(s p e) c -> p s (e c)", p=P, e=2),
-        )
         k_rows = keep.tile([P, ROW_TILES, HK * D], BF16)
         nc.sync.dma_start(out=k_rows[:], in_=k_view)
         q_rows = []
         for i in range(ROW_TILES):
             q_rows.append(q_pool.tile([P, H * D], BF16, name="q_rows"))
-        nc.sync.dma_start(out=q_rows[0][:], in_=q_view[:, 0, :])
-        x_rows = keep.tile([P, ROW_TILES, C], BF16)
         for half in range(2):
-            cols = slice(half * C // 2, (half + 1) * C // 2)
-            nc.sync.dma_start(out=x_rows[:, :, cols], in_=x_view[:, :, cols])
+            cols = slice(half * H * D // 2, (half + 1) * H * D // 2)
+            nc.sync.dma_start(out=q_rows[0][:, cols], in_=q_view[:, 0, cols])
+        w_rows = keep.tile([P, C * HK * D // P], BF16)
+        nc.sync.dma_start(
+            out=w_rows[:].rearrange("p (s f) -> p s f", s=2 * PASSES),
+            in_=Wv.rearrange("(s p e) c -> p s (e c)", p=P, e=2),
+        )
+        x_rows = []
+        for half in range(2):
+            x_rows.append(keep.tile([P, ROW_TILES, C // 2], BF16, name="x_rows_%d" % half))
+            nc.sync.dma_start(out=x_rows[half][:], in_=x_view[:, :, half * C // 2 : (half + 1) * C // 2])
         bias_rows = keep.tile([P, HK * D], BF16)
         nc.sync.dma_start(out=bias_rows[:], in_=bv.partition_broadcast(P))
         for i in range(1, ROW_TILES):
             nc.sync.dma_start(out=q_rows[i][:], in_=q_view[:, i, :])
 
-        def turn_blocks(blocks, grouped):
-            grouped_words = grouped.bitcast(F32).rearrange("p (b r u) -> p b r u", b=4, u=2)
-            for half in range(2):
-                turned = psum_turned.tile([P, 2, 2, P], F32, tag="turned")
-                for b in range(2):
-                    words = blocks[2 * half + b].bitcast(F32)
-                    for u in range(2):
-                        nc.tensor.transpose(turned[:, b, u, :], words[:, u * P : (u + 1) * P], ident_f32[:])
-                nc.scalar.copy(
-                    out=grouped_words[:, 2 * half : 2 * half + 2, :, :],
-                    in_=turned[:].rearrange("p b u r -> p b r u"),
-                )
+        warm_in = keep.tile([P, 1], F32)
+        nc.vector.memset(warm_in[:], 0.0)
+        warm_out = keep.tile([P, 1], F32)
+        nc.scalar.activation(out=warm_out[:], in_=warm_in[:], func=ACT.Exp)
+        ident_bf16 = keep.tile([P, P], BF16)
+        make_identity(nc, ident_bf16[:])
+        ident_f32 = keep.tile([P, P], F32)
+        make_identity(nc, ident_f32[:])
+
+        kT = []
+        for j in range(HK):
+            k_turned = psum_turned.tile([P, ROW_TILES, P], BF16, tag="turned")
+            for i in range(ROW_TILES):
+                nc.tensor.transpose(k_turned[:, i, :], k_rows[:, i, j * D : (j + 1) * D], ident_bf16[:])
+            kT.append(keep.tile([P, T], BF16, name="kT_%d" % j))
+            nc.vector.tensor_copy(
+                out=kT[j][:].rearrange("p (u r e) -> p u r e", u=2, e=2),
+                in_=k_turned[:].rearrange("p (u e) r -> p u r e", u=2),
+            )
+
+        qT = [[None, None] for i in range(ROW_TILES)]
+        q_turned = {}
+
+        def turn_queries(i, half):
+            q_turned[i, half] = psum_turned.tile([P, H // 2, P], BF16, tag="turned", name="q_turned")
+            for a in range(H // 2):
+                h = half * (H // 2) + a
+                nc.tensor.transpose(q_turned[i, half][:, a, :], q_rows[i][:, h * D : (h + 1) * D], ident_bf16[:])
+
+        def copy_queries(i, half):
+            qT[i][half] = qT_pool.tile([P, H // 2, P], BF16, name="qT_%d" % half)
+            nc.scalar.copy(out=qT[i][half][:], in_=q_turned[i, half][:])
 
         w_grouped = keep.tile([P, PASSES * HK * D * PACK], BF16, align_bytes=64)
         w_codes = keep.tile([P, PASSES, HK * D], U32, align_bytes=64)
         w_scales = keep.tile([P, PASSES, HK * D], U8, align_bytes=64)
-        per_pass = HK * D * PACK
-        for g in range(PASSES):
-            nc.vector.tensor_copy(
-                out=w_grouped[:, g * per_pass : (g + 1) * per_pass].rearrange("p (c t) -> p c t", t=PACK),
-                in_=w_rows[:, g * per_pass : (g + 1) * per_pass].rearrange("p (t c) -> p c t", t=PACK),
-            )
-        nc.vector.quantize_mx(
-            out=w_codes[:].rearrange("p g c -> p (g c)").bitcast(FP8X4),
-            scales=w_scales[:].rearrange("p g c -> p (g c)"),
-            in_=w_grouped[:],
-        )
-
-        kT = keep.tile([P, HK, T], BF16)
-        k_turned = psum_turned.tile([P, HK, ROW_TILES, P], BF16, tag="turned")
-        for j in range(HK):
-            for i in range(ROW_TILES):
-                nc.tensor.transpose(k_turned[:, j, i, :], k_rows[:, i, j * D : (j + 1) * D], ident_bf16[:])
-        nc.scalar.copy(
-            out=kT[:].rearrange("p j (u r e) -> p j u r e", u=2, e=2),
-            in_=k_turned[:].rearrange("p j (u e) r -> p j u r e", u=2),
-        )
-
-        qT = [None] * ROW_TILES
-
-        def turn_queries(i, half):
-            if half == 0:
-                qT[i] = qT_pool.tile([P, H, P], BF16, name="qT")
-            q_turned = psum_turned.tile([P, H // 2, P], BF16, tag="turned")
-            for a in range(H // 2):
-                h = half * (H // 2) + a
-                nc.tensor.transpose(q_turned[:, a, :], q_rows[i][:, h * D : (h + 1) * D], ident_bf16[:])
-            nc.scalar.copy(out=qT[i][:, half * (H // 2) : (half + 1) * (H // 2), :], in_=q_turned[:])
-
-        turn_queries(0, 0)
-        turn_queries(0, 1)
-
         x_codes = keep.tile([P, PASSES, T], U32, align_bytes=64)
         x_scales = keep.tile([P, PASSES, T], U8, align_bytes=64)
+        v_grouped = keep.tile([P, HK, D, PACK], BF16, align_bytes=64)
+        v_codes = []
+        v_scales = []
+        for j in range(HK):
+            v_codes.append(keep.tile([P, D], U32, align_bytes=64, name="v_codes_%d" % j))
+            v_scales.append(keep.tile([P, D], U8, align_bytes=64, name="v_scales_%d" % j))
+        x_turned = {}
+        x_grouped = {}
         v_sums = []
-        v_codes = keep.tile([P, HK * D], U32, align_bytes=64)
-        v_scales = keep.tile([P, HK * D], U8, align_bytes=64)
 
-        def quantise_x():
-            for g in range(PASSES):
-                x_grouped = x_pool.tile([P, 4 * K_PASS], BF16, align_bytes=64)
-                turn_blocks([x_rows[:, i, g * K_PASS : (g + 1) * K_PASS] for i in range(ROW_TILES)], x_grouped[:])
-                nc.vector.quantize_mx(
-                    out=x_codes[:, g, :].bitcast(FP8X4), scales=x_scales[:, g, :], in_=x_grouped[:]
-                )
-
-        def value_matmuls():
-            for j in range(HK):
-                v_sums.append(psum_sums.tile([P, ROW_TILES, D], F32, tag="sums", name="v_sums"))
-                for i in range(ROW_TILES):
-                    for g in range(PASSES):
-                        nc.tensor.matmul_mx(
-                            out=v_sums[j][:, i, :],
-                            lhsT=x_codes[:, g, i * P : (i + 1) * P].bitcast(FP8X4),
-                            lhsT_scale=x_scales[:, g, i * P : (i + 1) * P],
-                            rhs=w_codes[:, g, j * D : (j + 1) * D].bitcast(FP8X4),
-                            rhs_scale=w_scales[:, g, j * D : (j + 1) * D],
-                            start=(g == 0),
-                            stop=(g == PASSES - 1),
-                        )
-
-        def quantise_v():
-            v_grouped = keep.tile([P, HK, D, PACK], BF16, align_bytes=64)
-            for j in range(HK):
-                nc.vector.tensor_tensor(
-                    out=v_grouped[:, j, :, :],
-                    in0=v_sums[j][:].rearrange("p t c -> p c t"),
-                    in1=bias_rows[:, j * D : (j + 1) * D].unsqueeze(2).to_broadcast([P, D, PACK]),
-                    op=ALU.add,
-                )
-            nc.vector.quantize_mx(
-                out=v_codes[:].bitcast(FP8X4),
-                scales=v_scales[:],
-                in_=v_grouped[:].rearrange("p j c t -> p (j c t)"),
+        def group_w(g):
+            cols = slice(g * HK * D * PACK, (g + 1) * HK * D * PACK)
+            nc.gpsimd.tensor_scalar(
+                out=w_grouped[:, cols].rearrange("p (c t) -> p c t", t=PACK),
+                in0=w_rows[:, cols].rearrange("p (t c) -> p c t", t=PACK),
+                scalar1=1.0,
+                scalar2=0.0,
+                op0=ALU.mult,
+                op1=ALU.add,
             )
 
-        N = ROW_TILES * GROUPS
-        raw_scores = [None] * N
-        clipped = [None] * N
-        row_max = [None] * N
-        neg_max = [None] * N
-        row_sum = [None] * N
-        e_grouped = [None] * N
-        e_codes = [None] * N
-        e_scales = [None] * N
-        o_sums = [None] * N
+        def quantise_w():
+            nc.vector.quantize_mx(
+                out=w_codes[:].rearrange("p g c -> p (g c)").bitcast(FP8X4),
+                scales=w_scales[:].rearrange("p g c -> p (g c)"),
+                in_=w_grouped[:],
+            )
 
-        def kv_head(n):
-            return (n % GROUPS) * HEADS_PER_GROUP * HK // H
+        def turn_x(g, half):
+            x_turned[g, half] = psum_sums.tile([P, 2, 2, P], F32, tag="sums", name="x_turned")
+            for b in range(2):
+                part, k0 = divmod(g * K_PASS, C // 2)
+                words = x_rows[part][:, 2 * half + b, k0 : k0 + K_PASS].bitcast(F32)
+                for u in range(2):
+                    nc.tensor.transpose(x_turned[g, half][:, b, u, :], words[:, u * P : (u + 1) * P], ident_f32[:])
 
-        def score_matmuls(n):
-            i, hq = divmod(n, GROUPS)
-            raw_scores[n] = []
-            for a in range(HEADS_PER_GROUP):
-                s_raw = psum_scores.tile([P, T], F32)
+        def copy_x(g, half, copy):
+            if half == 0:
+                x_grouped[g] = x_pool.tile([P, 4 * K_PASS], BF16, align_bytes=64, name="x_grouped")
+            copy_turned(copy, x_grouped[g], half, x_turned[g, half])
+
+        def quantise_x(g):
+            nc.vector.quantize_mx(out=x_codes[:, g, :].bitcast(FP8X4), scales=x_scales[:, g, :], in_=x_grouped[g][:])
+
+        def value_matmuls(j):
+            v_sums.append(psum_sums.tile([P, ROW_TILES, D], F32, tag="sums", name="v_sums"))
+            for i in range(ROW_TILES):
+                for g in range(PASSES):
+                    nc.tensor.matmul_mx(
+                        out=v_sums[j][:, i, :],
+                        lhsT=x_codes[:, g, i * P : (i + 1) * P].bitcast(FP8X4),
+                        lhsT_scale=x_scales[:, g, i * P : (i + 1) * P],
+                        rhs=w_codes[:, g, j * D : (j + 1) * D].bitcast(FP8X4),
+                        rhs_scale=w_scales[:, g, j * D : (j + 1) * D],
+                        start=(g == 0),
+                        stop=(g == PASSES - 1),
+                    )
+
+        def add_bias(j):
+            nc.vector.tensor_tensor(
+                out=v_grouped[:, j, :, :],
+                in0=v_sums[j][:].rearrange("p t c -> p c t"),
+                in1=bias_rows[:, j * D : (j + 1) * D].unsqueeze(2).to_broadcast([P, D, PACK]),
+                op=ALU.add,
+            )
+
+        def quantise_v(j):
+            nc.vector.quantize_mx(
+                out=v_codes[j][:].bitcast(FP8X4),
+                scales=v_scales[j][:],
+                in_=v_grouped[:, j, :, :].rearrange("p c t -> p (c t)"),
+            )
+
+        M = ROW_TILES * PAIRS_PER_TILE
+        N = M // 2
+        raw_scores = {}
+        clipped = {}
+        row_max = {}
+        neg_max = {}
+        row_sum = {}
+        e_rows = {}
+        e_turned = {}
+        e_grouped = {}
+        e_codes = {}
+        e_scales = {}
+        o_sums = {}
+
+        def kv_head(m):
+            return (m % PAIRS_PER_TILE) * PAIR * HK // H
+
+        def score_matmuls(m):
+            i, b = divmod(m, PAIRS_PER_TILE)
+            half, b = divmod(b, PAIRS_PER_TILE // 2)
+            for a in range(PAIR):
+                raw_scores[m, a] = psum_scores.tile([P, T], F32, name="raw_scores")
                 nc.tensor.matmul(
-                    out=s_raw[:],
-                    lhsT=qT[i][:, hq * HEADS_PER_GROUP + a, :],
-                    rhs=kT[:, kv_head(n), :],
+                    out=raw_scores[m, a][:],
+                    lhsT=qT[i][half][:, b * PAIR + a, :],
+                    rhs=kT[kv_head(m)][:],
                     start=True,
                     stop=True,
                 )
-                raw_scores[n].append(s_raw)
 
-        def upper_clip_and_max(n):
-            row_max[n] = stats.tile([P, HEADS_PER_GROUP], F32, name="row_max")
-            clipped[n] = []
-            for a in range(HEADS_PER_GROUP):
-                s_clip = score_pool.tile([P, T], F32)
-                nc.vector.tensor_scalar(
-                    out=s_clip[:],
-                    in0=raw_scores[n][a][:],
-                    scalar1=RAW_CLIP,
-                    scalar2=-RAW_CLIP,
-                    op0=ALU.min,
-                    op1=ALU.max,
-                    accum_out=row_max[n][:, a : a + 1],
-                )
-                clipped[n].append(s_clip)
-                if a < GPSIMD_CLIPS:
-                    nc.gpsimd.tensor_scalar(
-                        out=s_clip[:],
-                        in0=s_clip[:],
-                        scalar1=RAW_CLIP,
-                        scalar2=-RAW_CLIP,
-                        op0=ALU.min,
-                        op1=ALU.max,
-                    )
+        def upper_clip_and_max(m, a):
+            if a == 0:
+                row_max[m] = stats.tile([P, PAIR], F32, name="row_max")
+            clipped[m, a] = score_pool.tile([P, T], F32, name="clipped")
+            nc.vector.tensor_scalar(
+                out=clipped[m, a][:],
+                in0=raw_scores[m, a][:],
+                scalar1=RAW_CLIP,
+                scalar2=-RAW_CLIP,
+                op0=ALU.min,
+                op1=ALU.max,
+                accum_out=row_max[m][:, a : a + 1],
+            )
 
-        def lower_clip_on_vector(n):
-            neg_max[n] = stats.tile([P, HEADS_PER_GROUP], F32, name="neg_max")
-            nc.vector.tensor_scalar_mul(out=neg_max[n][:], in0=row_max[n][:], scalar1=-SCALE)
-            for a in range(GPSIMD_CLIPS, HEADS_PER_GROUP):
-                nc.vector.tensor_scalar_max(out=clipped[n][a][:], in0=clipped[n][a][:], scalar1=-RAW_CLIP)
+        def lower_clip(m, a):
+            nc.gpsimd.tensor_scalar(
+                out=clipped[m, a][:],
+                in0=clipped[m, a][:],
+                scalar1=RAW_CLIP,
+                scalar2=-RAW_CLIP,
+                op0=ALU.min,
+                op1=ALU.max,
+            )
 
-        def exp_and_turn(n):
-            row_sum[n] = stats.tile([P, HEADS_PER_GROUP], F32, name="row_sum")
-            e_rows = work.tile([P, HEADS_PER_GROUP, T], BF16)
-            for a in range(HEADS_PER_GROUP):
-                nc.scalar.activation(
-                    out=e_rows[:, a, :],
-                    in_=clipped[n][a][:],
-                    func=ACT.Exp,
-                    bias=neg_max[n][:, a : a + 1],
-                    scale=SCALE,
-                    accum_out=row_sum[n][:, a : a + 1],
-                )
-            e_grouped[n] = work.tile([P, 4 * K_PASS], BF16, align_bytes=64, name="e_grouped")
-            turn_blocks([e_rows[:, a, :] for a in range(HEADS_PER_GROUP)], e_grouped[n][:])
+        def negate_max(m):
+            neg_max[m] = stats.tile([P, PAIR], F32, name="neg_max")
+            nc.gpsimd.tensor_scalar(
+                out=neg_max[m][:], in0=row_max[m][:], scalar1=-SCALE, scalar2=0.0, op0=ALU.mult, op1=ALU.add
+            )
+
+        def exp(m, a):
+            n, odd = divmod(m, 2)
+            if odd == 0 and a == 0:
+                row_sum[n] = stats.tile([P, GROUP], F32, name="row_sum")
+            if a == 0:
+                e_rows[m] = work.tile([P, PAIR, T], BF16, name="e_rows")
+            h = odd * PAIR + a
+            nc.scalar.activation(
+                out=e_rows[m][:, a, :],
+                in_=clipped[m, a][:],
+                func=ACT.Exp,
+                bias=neg_max[m][:, a : a + 1],
+                scale=SCALE,
+                accum_out=row_sum[n][:, h : h + 1],
+            )
+
+        def turn_e(m, a):
+            if a == 0:
+                e_turned[m] = psum_turned.tile([P, PAIR, 2, P], F32, tag="turned", name="e_turned")
+            words = e_rows[m][:, a, :].bitcast(F32)
+            for u in range(2):
+                nc.tensor.transpose(e_turned[m][:, a, u, :], words[:, u * P : (u + 1) * P], ident_f32[:])
+
+        def copy_turned(copy, grouped, half, turned):
+            words = grouped[:].bitcast(F32).rearrange("p (b r u) -> p b r u", b=4, u=2)
+            copy(
+                out=words[:, 2 * half : 2 * half + 2, :, :],
+                in_=turned[:].rearrange("p b u r -> p b r u"),
+            )
+
+        def copy_e(m):
+            n, odd = divmod(m, 2)
+            if odd == 0:
+                e_grouped[n] = work.tile([P, 4 * K_PASS], BF16, align_bytes=64, name="e_grouped")
+            copy_turned(nc.scalar.copy, e_grouped[n], odd, e_turned[m])
 
         def quantise_e(n):
-            e_codes[n] = work.tile([P, HEADS_PER_GROUP * P], U32, align_bytes=64, name="e_codes")
-            e_scales[n] = work.tile([P, HEADS_PER_GROUP * P], U8, align_bytes=64, name="e_scales")
+            e_codes[n] = work.tile([P, GROUP * P], U32, align_bytes=64, name="e_codes")
+            e_scales[n] = work.tile([P, GROUP * P], U8, align_bytes=64, name="e_scales")
             nc.vector.quantize_mx(out=e_codes[n][:].bitcast(FP8X4), scales=e_scales[n][:], in_=e_grouped[n][:])
 
         def weighted_sums(n):
-            j = kv_head(n)
-            o_sums[n] = psum_sums.tile([P, HEADS_PER_GROUP, D], F32, tag="sums", name="o_sums")
-            for a in range(HEADS_PER_GROUP):
+            j = kv_head(2 * n)
+            o_sums[n] = psum_sums.tile([P, GROUP, D], F32, tag="sums", name="o_sums")
+            for a in range(GROUP):
                 nc.tensor.matmul_mx(
                     out=o_sums[n][:, a, :],
                     lhsT=e_codes[n][:, a * P : (a + 1) * P].bitcast(FP8X4),
                     lhsT_scale=e_scales[n][:, a * P : (a + 1) * P],
-                    rhs=v_codes[:, j * D : (j + 1) * D].bitcast(FP8X4),
-                    rhs_scale=v_scales[:, j * D : (j + 1) * D],
+                    rhs=v_codes[j][:].bitcast(FP8X4),
+                    rhs_scale=v_scales[j][:],
                     start=True,
                     stop=True,
                 )
 
-        def normalise_and_store(n):
-            i, hq = divmod(n, GROUPS)
-            inv_sum = stats.tile([P, HEADS_PER_GROUP], F32)
+        def normalise_and_store(n, on_scalar):
+            i, hq = divmod(n, H // GROUP)
+            inv_sum = stats.tile([P, GROUP], F32)
             nc.vector.reciprocal(out=inv_sum[:], in_=row_sum[n][:])
-            o_rows = work.tile([P, HEADS_PER_GROUP, D], F32)
-            nc.vector.tensor_tensor(
-                out=o_rows[:],
-                in0=o_sums[n][:],
-                in1=inv_sum[:].unsqueeze(2).to_broadcast([P, HEADS_PER_GROUP, D]),
-                op=ALU.mult,
-            )
-            cols = slice(hq * HEADS_PER_GROUP * D, (hq + 1) * HEADS_PER_GROUP * D)
+            o_rows = work.tile([P, GROUP, D], F32)
+            if on_scalar:
+                for a in range(GROUP):
+                    nc.scalar.mul(out=o_rows[:, a, :], in_=o_sums[n][:, a, :], mul=inv_sum[:, a : a + 1])
+            else:
+                nc.vector.tensor_tensor(
+                    out=o_rows[:],
+                    in0=o_sums[n][:],
+                    in1=inv_sum[:].unsqueeze(2).to_broadcast([P, GROUP, D]),
+                    op=ALU.mult,
+                )
+            cols = slice(hq * GROUP * D, (hq + 1) * GROUP * D)
             nc.sync.dma_start(out=out_view[:, i, cols], in_=o_rows[:].rearrange("p a d -> p (a d)"))
 
+        X_START = 2
+        VALUES_READY = 2 + 6
+        attend_step = [max(2 * n + 8, VALUES_READY + n) for n in range(N)]
+
+        for half in range(2):
+            turn_queries(0, half)
+            copy_queries(0, half)
         score_matmuls(0)
-        for n in range(N + 4):
-            if n < N:
-                upper_clip_and_max(n)
-            if 0 <= n - 4:
-                normalise_and_store(n - 4)
-            if n < N:
-                lower_clip_on_vector(n)
-            if n == 2:
-                quantise_v()
-            if 0 <= n - 2 < N:
-                quantise_e(n - 2)
-            if 0 <= n - 3 < N:
-                weighted_sums(n - 3)
-            if 0 <= n - 1 < N:
-                exp_and_turn(n - 1)
-            if n == 0:
-                quantise_x()
-            if n == 1:
-                value_matmuls()
-            if n // GROUPS + 1 < ROW_TILES and n % GROUPS in (1, 2):
-                turn_queries(n // GROUPS + 1, n % GROUPS - 1)
-            if n + 1 < N:
-                score_matmuls(n + 1)
+        for s in range(attend_step[N - 1] + 1 + 2):
+            if s + 1 < M:
+                score_matmuls(s + 1)
+            for n in range(N):
+                if attend_step[n] == s:
+                    weighted_sums(n)
+            if s < M:
+                upper_clip_and_max(s, 0)
+                lower_clip(s, 0)
+            if s >= 7 and (s - 7) % 2 == 0 and (s - 7) // 2 < N:
+                quantise_e((s - 7) // 2)
+            if s < M:
+                upper_clip_and_max(s, 1)
+                lower_clip(s, 1)
+                negate_max(s)
+            g = s - X_START
+            if 1 <= g < 1 + PASSES:
+                copy_x(g - 1, 0, nc.vector.tensor_copy)
+            for n in range(N):
+                if attend_step[n] == s - 2:
+                    normalise_and_store(n, False)
+
+            i, b = divmod(s, PAIRS_PER_TILE)
+            turning = i + 1 < ROW_TILES and b in (3, 3 + 2)
+            if turning:
+                turn_queries(i + 1, (b - 3) // 2)
+
+            m = s - 2
+            if 0 <= m < M:
+                exp(m, 0)
+            if 0 <= m - 1 < M:
+                copy_e(m - 1)
+            if 1 <= g < 1 + PASSES:
+                copy_x(g - 1, 1, nc.scalar.copy)
+            if 0 <= m < M:
+                turn_e(m, 0)
+                exp(m, 1)
+                turn_e(m, 1)
+            if turning:
+                copy_queries(i + 1, (b - 3) // 2)
+
+            if 0 <= g < PASSES:
+                turn_x(g, 0)
+                turn_x(g, 1)
+
+            if 1 <= s < 1 + PASSES:
+                group_w(s - 1)
+            if s == 5:
+                quantise_w()
+            if 2 <= g < 2 + PASSES:
+                quantise_x(g - 2)
+            if g == PASSES + 1:
+                value_matmuls(0)
+                value_matmuls(1)
+                add_bias(0)
+                quantise_v(0)
+                add_bias(1)
+                quantise_v(1)

@@ -41,7 +41,7 @@ def tile_multiqueryattention_pa_kernel(tc, x, Wv, bv, q, k, out):
         keep = ctx.enter_context(tc.tile_pool(name="keep", bufs=1))
         q_pool = ctx.enter_context(tc.tile_pool(name="q_pool", bufs=ROW_TILES))
         qT_pool = ctx.enter_context(tc.tile_pool(name="qT_pool", bufs=2))
-        score_pool = ctx.enter_context(tc.tile_pool(name="score_pool", bufs=4 * PAIR))
+        score_pool = ctx.enter_context(tc.tile_pool(name="score_pool", bufs=4))
         x_pool = ctx.enter_context(tc.tile_pool(name="x_pool", bufs=PASSES))
         work = ctx.enter_context(tc.tile_pool(name="work", bufs=6))
         stats = ctx.enter_context(tc.tile_pool(name="stats", bufs=16))
@@ -126,13 +126,9 @@ def tile_multiqueryattention_pa_kernel(tc, x, Wv, bv, q, k, out):
 
         def group_w(g):
             cols = slice(g * HK * D * PACK, (g + 1) * HK * D * PACK)
-            nc.gpsimd.tensor_scalar(
+            nc.vector.tensor_copy(
                 out=w_grouped[:, cols].rearrange("p (c t) -> p c t", t=PACK),
-                in0=w_rows[:, cols].rearrange("p (t c) -> p c t", t=PACK),
-                scalar1=1.0,
-                scalar2=0.0,
-                op0=ALU.mult,
-                op1=ALU.add,
+                in_=w_rows[:, cols].rearrange("p (t c) -> p c t", t=PACK),
             )
 
         def quantise_w():
@@ -220,9 +216,9 @@ def tile_multiqueryattention_pa_kernel(tc, x, Wv, bv, q, k, out):
         def upper_clip_and_max(m, a):
             if a == 0:
                 row_max[m] = stats.tile([P, PAIR], F32, name="row_max")
-            clipped[m, a] = score_pool.tile([P, T], F32, name="clipped")
+                clipped[m] = score_pool.tile([P, PAIR, T], F32, name="clipped")
             nc.vector.tensor_scalar(
-                out=clipped[m, a][:],
+                out=clipped[m][:, a, :],
                 in0=raw_scores[m, a][:],
                 scalar1=RAW_CLIP,
                 scalar2=-RAW_CLIP,
@@ -231,10 +227,11 @@ def tile_multiqueryattention_pa_kernel(tc, x, Wv, bv, q, k, out):
                 accum_out=row_max[m][:, a : a + 1],
             )
 
-        def lower_clip(m, a):
+        def lower_clip(m):
+            pair = clipped[m][:].rearrange("p a k -> p (a k)")
             nc.gpsimd.tensor_scalar(
-                out=clipped[m, a][:],
-                in0=clipped[m, a][:],
+                out=pair,
+                in0=pair,
                 scalar1=RAW_CLIP,
                 scalar2=-RAW_CLIP,
                 op0=ALU.min,
@@ -243,9 +240,7 @@ def tile_multiqueryattention_pa_kernel(tc, x, Wv, bv, q, k, out):
 
         def negate_max(m):
             neg_max[m] = stats.tile([P, PAIR], F32, name="neg_max")
-            nc.gpsimd.tensor_scalar(
-                out=neg_max[m][:], in0=row_max[m][:], scalar1=-SCALE, scalar2=0.0, op0=ALU.mult, op1=ALU.add
-            )
+            nc.scalar.mul(out=neg_max[m][:], in_=row_max[m][:], mul=-SCALE)
 
         def exp(m, a):
             n, odd = divmod(m, 2)
@@ -256,7 +251,7 @@ def tile_multiqueryattention_pa_kernel(tc, x, Wv, bv, q, k, out):
             h = odd * PAIR + a
             nc.scalar.activation(
                 out=e_rows[m][:, a, :],
-                in_=clipped[m, a][:],
+                in_=clipped[m][:, a, :],
                 func=ACT.Exp,
                 bias=neg_max[m][:, a : a + 1],
                 scale=SCALE,
@@ -336,13 +331,11 @@ def tile_multiqueryattention_pa_kernel(tc, x, Wv, bv, q, k, out):
                     weighted_sums(n)
             if s < M:
                 upper_clip_and_max(s, 0)
-                lower_clip(s, 0)
-            if s >= 7 and (s - 7) % 2 == 0 and (s - 7) // 2 < N:
-                quantise_e((s - 7) // 2)
             if s < M:
                 upper_clip_and_max(s, 1)
-                lower_clip(s, 1)
-                negate_max(s)
+                lower_clip(s)
+            if s >= 7 and (s - 7) % 2 == 0 and (s - 7) // 2 < N:
+                quantise_e((s - 7) // 2)
             g = s - X_START
             if 1 <= g < 1 + PASSES:
                 copy_x(g - 1, 0, nc.vector.tensor_copy)
@@ -357,6 +350,7 @@ def tile_multiqueryattention_pa_kernel(tc, x, Wv, bv, q, k, out):
 
             m = s - 2
             if 0 <= m < M:
+                negate_max(m)
                 exp(m, 0)
             if 0 <= m - 1 < M:
                 copy_e(m - 1)

@@ -25,7 +25,7 @@ ROW_TILES = T // P
 PASSES = C // K_PASS
 PAIR = 2
 GROUP = 4
-PAIRS_PER_TILE = H // PAIR
+GROUPS = H // GROUP
 
 SCALE = 1.0 / math.sqrt(D)
 CLIP = 100.0
@@ -43,7 +43,9 @@ def tile_multiqueryattention_pa_kernel(tc, x, Wv, bv, q, k, out):
         qT_pool = ctx.enter_context(tc.tile_pool(name="qT_pool", bufs=2))
         score_pool = ctx.enter_context(tc.tile_pool(name="score_pool", bufs=4))
         x_pool = ctx.enter_context(tc.tile_pool(name="x_pool", bufs=PASSES))
-        work = ctx.enter_context(tc.tile_pool(name="work", bufs=6))
+        e_pool = ctx.enter_context(tc.tile_pool(name="e_pool", bufs=4))
+        code_pool = ctx.enter_context(tc.tile_pool(name="code_pool", bufs=5))
+        out_pool = ctx.enter_context(tc.tile_pool(name="out_pool", bufs=4))
         stats = ctx.enter_context(tc.tile_pool(name="stats", bufs=16))
         psum_scores = ctx.enter_context(tc.psum_pool(name="psum_scores", bufs=2 * PAIR))
         psum_turned = ctx.enter_context(tc.psum_pool(name="psum_turned", bufs=2))
@@ -124,9 +126,9 @@ def tile_multiqueryattention_pa_kernel(tc, x, Wv, bv, q, k, out):
         x_grouped = {}
         v_sums = []
 
-        def group_w(g):
+        def group_w(g, copy):
             cols = slice(g * HK * D * PACK, (g + 1) * HK * D * PACK)
-            nc.vector.tensor_copy(
+            copy(
                 out=w_grouped[:, cols].rearrange("p (c t) -> p c t", t=PACK),
                 in_=w_rows[:, cols].rearrange("p (t c) -> p c t", t=PACK),
             )
@@ -183,13 +185,13 @@ def tile_multiqueryattention_pa_kernel(tc, x, Wv, bv, q, k, out):
                 in_=v_grouped[:, j, :, :].rearrange("p c t -> p (c t)"),
             )
 
-        M = ROW_TILES * PAIRS_PER_TILE
-        N = M // 2
+        N = ROW_TILES * GROUPS
         raw_scores = {}
         clipped = {}
         row_max = {}
         neg_max = {}
         row_sum = {}
+        inv_sum = {}
         e_rows = {}
         e_turned = {}
         e_grouped = {}
@@ -197,73 +199,67 @@ def tile_multiqueryattention_pa_kernel(tc, x, Wv, bv, q, k, out):
         e_scales = {}
         o_sums = {}
 
-        def kv_head(m):
-            return (m % PAIRS_PER_TILE) * PAIR * HK // H
+        def kv_head(n):
+            return (n % GROUPS) * GROUP * HK // H
 
-        def score_matmuls(m):
-            i, b = divmod(m, PAIRS_PER_TILE)
-            half, b = divmod(b, PAIRS_PER_TILE // 2)
-            for a in range(PAIR):
-                raw_scores[m, a] = psum_scores.tile([P, T], F32, name="raw_scores")
-                nc.tensor.matmul(
-                    out=raw_scores[m, a][:],
-                    lhsT=qT[i][half][:, b * PAIR + a, :],
-                    rhs=kT[kv_head(m)][:],
-                    start=True,
-                    stop=True,
-                )
+        def score_matmul(n, a):
+            i, hq = divmod(n, GROUPS)
+            half, h = divmod(hq * GROUP + a, H // 2)
+            raw_scores[n, a] = psum_scores.tile([P, T], F32, name="raw_scores")
+            nc.tensor.matmul(
+                out=raw_scores[n, a][:], lhsT=qT[i][half][:, h, :], rhs=kT[kv_head(n)][:], start=True, stop=True
+            )
 
-        def upper_clip_and_max(m, a):
+        def upper_clip_and_max(n, a):
+            b, odd = divmod(a, PAIR)
             if a == 0:
-                row_max[m] = stats.tile([P, PAIR], F32, name="row_max")
-                clipped[m] = score_pool.tile([P, PAIR, T], F32, name="clipped")
+                row_max[n] = stats.tile([P, GROUP], F32, name="row_max")
+            if odd == 0:
+                clipped[n, b] = score_pool.tile([P, PAIR, T], F32, name="clipped")
             nc.vector.tensor_scalar(
-                out=clipped[m][:, a, :],
-                in0=raw_scores[m, a][:],
+                out=clipped[n, b][:, odd, :],
+                in0=raw_scores[n, a][:],
                 scalar1=RAW_CLIP,
                 scalar2=-RAW_CLIP,
                 op0=ALU.min,
                 op1=ALU.max,
-                accum_out=row_max[m][:, a : a + 1],
+                accum_out=row_max[n][:, a : a + 1],
             )
 
-        def lower_clip(m):
-            pair = clipped[m][:].rearrange("p a k -> p (a k)")
-            nc.gpsimd.tensor_scalar(
-                out=pair,
-                in0=pair,
-                scalar1=RAW_CLIP,
-                scalar2=-RAW_CLIP,
-                op0=ALU.min,
-                op1=ALU.max,
+        def lower_clip(n, b, engine):
+            pair = clipped[n, b][:].rearrange("p a k -> p (a k)")
+            engine.tensor_scalar(
+                out=pair, in0=pair, scalar1=RAW_CLIP, scalar2=-RAW_CLIP, op0=ALU.min, op1=ALU.max
             )
 
-        def negate_max(m):
-            neg_max[m] = stats.tile([P, PAIR], F32, name="neg_max")
-            nc.scalar.mul(out=neg_max[m][:], in_=row_max[m][:], mul=-SCALE)
+        def negate_max(n, b):
+            if b == 0:
+                neg_max[n] = stats.tile([P, GROUP], F32, name="neg_max")
+            cols = slice(b * PAIR, (b + 1) * PAIR)
+            nc.scalar.mul(out=neg_max[n][:, cols], in_=row_max[n][:, cols], mul=-SCALE)
 
-        def exp(m, a):
-            n, odd = divmod(m, 2)
-            if odd == 0 and a == 0:
+        def exp(n, a):
+            b, odd = divmod(a, PAIR)
+            if a == 0:
                 row_sum[n] = stats.tile([P, GROUP], F32, name="row_sum")
-            if a == 0:
-                e_rows[m] = work.tile([P, PAIR, T], BF16, name="e_rows")
-            h = odd * PAIR + a
+            if odd == 0:
+                e_rows[n, b] = e_pool.tile([P, PAIR, T], BF16, name="e_rows")
             nc.scalar.activation(
-                out=e_rows[m][:, a, :],
-                in_=clipped[m][:, a, :],
+                out=e_rows[n, b][:, odd, :],
+                in_=clipped[n, b][:, odd, :],
                 func=ACT.Exp,
-                bias=neg_max[m][:, a : a + 1],
+                bias=neg_max[n][:, a : a + 1],
                 scale=SCALE,
-                accum_out=row_sum[n][:, h : h + 1],
+                accum_out=row_sum[n][:, a : a + 1],
             )
 
-        def turn_e(m, a):
-            if a == 0:
-                e_turned[m] = psum_turned.tile([P, PAIR, 2, P], F32, tag="turned", name="e_turned")
-            words = e_rows[m][:, a, :].bitcast(F32)
+        def turn_e(n, a):
+            b, odd = divmod(a, PAIR)
+            if odd == 0:
+                e_turned[n, b] = psum_turned.tile([P, PAIR, 2, P], F32, tag="turned", name="e_turned")
+            words = e_rows[n, b][:, odd, :].bitcast(F32)
             for u in range(2):
-                nc.tensor.transpose(e_turned[m][:, a, u, :], words[:, u * P : (u + 1) * P], ident_f32[:])
+                nc.tensor.transpose(e_turned[n, b][:, odd, u, :], words[:, u * P : (u + 1) * P], ident_f32[:])
 
         def copy_turned(copy, grouped, half, turned):
             words = grouped[:].bitcast(F32).rearrange("p (b r u) -> p b r u", b=4, u=2)
@@ -272,19 +268,18 @@ def tile_multiqueryattention_pa_kernel(tc, x, Wv, bv, q, k, out):
                 in_=turned[:].rearrange("p b u r -> p b r u"),
             )
 
-        def copy_e(m):
-            n, odd = divmod(m, 2)
-            if odd == 0:
-                e_grouped[n] = work.tile([P, 4 * K_PASS], BF16, align_bytes=64, name="e_grouped")
-            copy_turned(nc.scalar.copy, e_grouped[n], odd, e_turned[m])
+        def copy_e(n, b, copy):
+            if b == 0:
+                e_grouped[n] = e_pool.tile([P, 4 * K_PASS], BF16, align_bytes=64, name="e_grouped")
+            copy_turned(copy, e_grouped[n], b, e_turned[n, b])
 
         def quantise_e(n):
-            e_codes[n] = work.tile([P, GROUP * P], U32, align_bytes=64, name="e_codes")
-            e_scales[n] = work.tile([P, GROUP * P], U8, align_bytes=64, name="e_scales")
+            e_codes[n] = code_pool.tile([P, GROUP * P], U32, align_bytes=64, name="e_codes")
+            e_scales[n] = code_pool.tile([P, GROUP * P], U8, align_bytes=64, name="e_scales")
             nc.vector.quantize_mx(out=e_codes[n][:].bitcast(FP8X4), scales=e_scales[n][:], in_=e_grouped[n][:])
 
         def weighted_sums(n):
-            j = kv_head(2 * n)
+            j = kv_head(n)
             o_sums[n] = psum_sums.tile([P, GROUP, D], F32, tag="sums", name="o_sums")
             for a in range(GROUP):
                 nc.tensor.matmul_mx(
@@ -297,83 +292,106 @@ def tile_multiqueryattention_pa_kernel(tc, x, Wv, bv, q, k, out):
                     stop=True,
                 )
 
+        def invert_sums(n):
+            inv_sum[n] = stats.tile([P, GROUP], F32, name="inv_sum")
+            nc.vector.reciprocal(out=inv_sum[n][:], in_=row_sum[n][:])
+
         def normalise_and_store(n, on_scalar):
-            i, hq = divmod(n, H // GROUP)
-            inv_sum = stats.tile([P, GROUP], F32)
-            nc.vector.reciprocal(out=inv_sum[:], in_=row_sum[n][:])
-            o_rows = work.tile([P, GROUP, D], F32)
+            i, hq = divmod(n, GROUPS)
+            o_rows = out_pool.tile([P, GROUP, D], F32)
             if on_scalar:
                 for a in range(GROUP):
-                    nc.scalar.mul(out=o_rows[:, a, :], in_=o_sums[n][:, a, :], mul=inv_sum[:, a : a + 1])
+                    nc.scalar.mul(out=o_rows[:, a, :], in_=o_sums[n][:, a, :], mul=inv_sum[n][:, a : a + 1])
             else:
                 nc.vector.tensor_tensor(
                     out=o_rows[:],
                     in0=o_sums[n][:],
-                    in1=inv_sum[:].unsqueeze(2).to_broadcast([P, GROUP, D]),
+                    in1=inv_sum[n][:].unsqueeze(2).to_broadcast([P, GROUP, D]),
                     op=ALU.mult,
                 )
             cols = slice(hq * GROUP * D, (hq + 1) * GROUP * D)
             nc.sync.dma_start(out=out_view[:, i, cols], in_=o_rows[:].rearrange("p a d -> p (a d)"))
 
-        X_START = 2
-        VALUES_READY = 2 + 6
-        attend_step = [max(2 * n + 8, VALUES_READY + n) for n in range(N)]
-
         for half in range(2):
             turn_queries(0, half)
             copy_queries(0, half)
-        score_matmuls(0)
-        for s in range(attend_step[N - 1] + 1 + 2):
-            if s + 1 < M:
-                score_matmuls(s + 1)
-            for n in range(N):
-                if attend_step[n] == s:
-                    weighted_sums(n)
-            if s < M:
-                upper_clip_and_max(s, 0)
-            if s < M:
-                upper_clip_and_max(s, 1)
-                lower_clip(s)
-            if s >= 7 and (s - 7) % 2 == 0 and (s - 7) // 2 < N:
-                quantise_e((s - 7) // 2)
-            g = s - X_START
-            if 1 <= g < 1 + PASSES:
-                copy_x(g - 1, 0, nc.vector.tensor_copy)
-            for n in range(N):
-                if attend_step[n] == s - 2:
-                    normalise_and_store(n, False)
+        for a in range(GROUP):
+            score_matmul(0, a)
 
-            i, b = divmod(s, PAIRS_PER_TILE)
-            turning = i + 1 < ROW_TILES and b in (3, 3 + 2)
-            if turning:
-                turn_queries(i + 1, (b - 3) // 2)
+        attend_step = [max(n + 3, 3 + n // 2) for n in range(N)]
+        for n in range(attend_step[N - 1] + 2):
+            done = [m for m in range(N) if attend_step[m] == n - 1]
+            now = [m for m in range(N) if attend_step[m] == n]
+            i, hq = divmod(n, GROUPS)
+            turning = i + 1 < ROW_TILES and hq in (1, 2)
+            if n < N:
+                upper_clip_and_max(n, 0)
+            for m in done:
+                if m % 2 == 0:
+                    normalise_and_store(m, False)
+            if 0 <= n - 3 < N:
+                invert_sums(n - 3)
+                quantise_e(n - 3)
+            if 0 <= n - 1 < N:
+                lower_clip(n - 1, 1, nc.vector)
+            if n < N:
+                upper_clip_and_max(n, 1)
+                lower_clip(n, 0, nc.gpsimd)
+                upper_clip_and_max(n, 2)
+                upper_clip_and_max(n, 3)
 
-            m = s - 2
-            if 0 <= m < M:
-                negate_max(m)
+            m = n - 1
+            if 0 <= m < N:
+                if m == 0:
+                    negate_max(m, 0)
                 exp(m, 0)
-            if 0 <= m - 1 < M:
-                copy_e(m - 1)
-            if 1 <= g < 1 + PASSES:
-                copy_x(g - 1, 1, nc.scalar.copy)
-            if 0 <= m < M:
                 turn_e(m, 0)
+            if 0 <= m - 1 < N:
+                copy_e(m - 1, 1, nc.scalar.copy)
+            if n + 1 < N:
+                score_matmul(n + 1, 0)
+            if 0 <= m < N:
+                negate_max(m, 1)
                 exp(m, 1)
                 turn_e(m, 1)
+            for d in done:
+                if not (d % 2 == 0):
+                    normalise_and_store(d, True)
+            if n + 1 < N:
+                score_matmul(n + 1, 1)
+            for d in now:
+                weighted_sums(d)
             if turning:
-                copy_queries(i + 1, (b - 3) // 2)
+                turn_queries(i + 1, hq - 1)
+            if 0 <= m < N:
+                exp(m, 2)
+                copy_e(m, 0, nc.scalar.copy)
+                turn_e(m, 2)
+            if n + 1 < N:
+                score_matmul(n + 1, 2)
+            if n < N and n > 0:
+                negate_max(n, 0)
+            if 0 <= m < N:
+                exp(m, 3)
+                turn_e(m, 3)
+            if n + 1 < N:
+                score_matmul(n + 1, 3)
+            if turning:
+                copy_queries(i + 1, hq - 1)
 
-            if 0 <= g < PASSES:
-                turn_x(g, 0)
-                turn_x(g, 1)
-
-            if 1 <= s < 1 + PASSES:
-                group_w(s - 1)
-            if s == 5:
+            if n == 0:
+                for g in range(2):
+                    group_w(g, nc.vector.tensor_copy)
+                    group_w(2 + g, nc.scalar.copy)
                 quantise_w()
-            if 2 <= g < 2 + PASSES:
-                quantise_x(g - 2)
-            if g == PASSES + 1:
+            if n in (0, 0 + 1):
+                for g in (2 * (n - 0), 2 * (n - 0) + 1):
+                    turn_x(g, 0)
+                    turn_x(g, 1)
+                    copy_x(g, 0, nc.vector.tensor_copy)
+                    copy_x(g, 1, nc.scalar.copy)
+                    quantise_x(g)
+            if n == 0 + 1:
                 value_matmuls(0)
                 value_matmuls(1)
                 add_bias(0)

@@ -26,6 +26,7 @@ PASSES = C // K_PASS
 PAIR = 2
 GROUP = 4
 GROUPS = H // GROUP
+VECTOR_HEADS = 3
 
 SCALE = 1.0 / math.sqrt(D)
 CLIP = 100.0
@@ -41,9 +42,9 @@ def tile_multiqueryattention_pa_kernel(tc, x, Wv, bv, q, k, out):
         keep = ctx.enter_context(tc.tile_pool(name="keep", bufs=1))
         q_pool = ctx.enter_context(tc.tile_pool(name="q_pool", bufs=ROW_TILES))
         qT_pool = ctx.enter_context(tc.tile_pool(name="qT_pool", bufs=2))
-        score_pool = ctx.enter_context(tc.tile_pool(name="score_pool", bufs=4))
+        score_pool = ctx.enter_context(tc.tile_pool(name="score_pool", bufs=8))
         x_pool = ctx.enter_context(tc.tile_pool(name="x_pool", bufs=PASSES))
-        e_pool = ctx.enter_context(tc.tile_pool(name="e_pool", bufs=4))
+        e_pool = ctx.enter_context(tc.tile_pool(name="e_pool", bufs=6))
         code_pool = ctx.enter_context(tc.tile_pool(name="code_pool", bufs=5))
         out_pool = ctx.enter_context(tc.tile_pool(name="out_pool", bufs=4))
         stats = ctx.enter_context(tc.tile_pool(name="stats", bufs=16))
@@ -61,22 +62,28 @@ def tile_multiqueryattention_pa_kernel(tc, x, Wv, bv, q, k, out):
         q_rows = []
         for i in range(ROW_TILES):
             q_rows.append(q_pool.tile([P, H * D], BF16, name="q_rows"))
+
+        def load_queries(i, first, end):
+            cols = slice(first * GROUP * D, end * GROUP * D)
+            nc.sync.dma_start(out=q_rows[i][:, cols], in_=q_view[:, i, cols])
+
+        load_queries(0, 0, 1)
+        x_rows = []
         for half in range(2):
-            cols = slice(half * H * D // 2, (half + 1) * H * D // 2)
-            nc.sync.dma_start(out=q_rows[0][:, cols], in_=q_view[:, 0, cols])
+            x_rows.append(keep.tile([P, ROW_TILES, C // 2], BF16, name="x_rows_%d" % half))
+            nc.sync.dma_start(out=x_rows[half][:], in_=x_view[:, :, half * C // 2 : (half + 1) * C // 2])
+            if half == 0:
+                load_queries(0, 1, 2)
         w_rows = keep.tile([P, C * HK * D // P], BF16)
         nc.sync.dma_start(
             out=w_rows[:].rearrange("p (s f) -> p s f", s=2 * PASSES),
             in_=Wv.rearrange("(s p e) c -> p s (e c)", p=P, e=2),
         )
-        x_rows = []
-        for half in range(2):
-            x_rows.append(keep.tile([P, ROW_TILES, C // 2], BF16, name="x_rows_%d" % half))
-            nc.sync.dma_start(out=x_rows[half][:], in_=x_view[:, :, half * C // 2 : (half + 1) * C // 2])
+        load_queries(0, 2, GROUPS)
         bias_rows = keep.tile([P, HK * D], BF16)
         nc.sync.dma_start(out=bias_rows[:], in_=bv.partition_broadcast(P))
         for i in range(1, ROW_TILES):
-            nc.sync.dma_start(out=q_rows[i][:], in_=q_view[:, i, :])
+            load_queries(i, 0, GROUPS)
 
         warm_in = keep.tile([P, 1], F32)
         nc.vector.memset(warm_in[:], 0.0)
@@ -87,29 +94,36 @@ def tile_multiqueryattention_pa_kernel(tc, x, Wv, bv, q, k, out):
         ident_f32 = keep.tile([P, P], F32)
         make_identity(nc, ident_f32[:])
 
-        kT = []
-        for j in range(HK):
-            k_turned = psum_turned.tile([P, ROW_TILES, P], BF16, tag="turned")
+        kT = [None] * HK
+        k_turned = [None] * HK
+
+        def turn_keys(j):
+            k_turned[j] = psum_turned.tile([P, ROW_TILES, P], BF16, tag="turned", name="k_turned")
             for i in range(ROW_TILES):
-                nc.tensor.transpose(k_turned[:, i, :], k_rows[:, i, j * D : (j + 1) * D], ident_bf16[:])
-            kT.append(keep.tile([P, T], BF16, name="kT_%d" % j))
+                nc.tensor.transpose(k_turned[j][:, i, :], k_rows[:, i, j * D : (j + 1) * D], ident_bf16[:])
+
+        def copy_keys(j):
+            kT[j] = keep.tile([P, T], BF16, name="kT_%d" % j)
             nc.vector.tensor_copy(
                 out=kT[j][:].rearrange("p (u r e) -> p u r e", u=2, e=2),
-                in_=k_turned[:].rearrange("p (u e) r -> p u r e", u=2),
+                in_=k_turned[j][:].rearrange("p (u e) r -> p u r e", u=2),
             )
 
-        qT = [[None, None] for i in range(ROW_TILES)]
+        qT = {}
         q_turned = {}
 
-        def turn_queries(i, half):
-            q_turned[i, half] = psum_turned.tile([P, H // 2, P], BF16, tag="turned", name="q_turned")
-            for a in range(H // 2):
-                h = half * (H // 2) + a
-                nc.tensor.transpose(q_turned[i, half][:, a, :], q_rows[i][:, h * D : (h + 1) * D], ident_bf16[:])
+        def turn_queries(n, count):
+            i, hq = divmod(n, GROUPS)
+            q_turned[n] = psum_sums.tile([P, count * GROUP, P], BF16, tag="sums", name="q_turned")
+            for a in range(count * GROUP):
+                h = hq * GROUP + a
+                nc.tensor.transpose(q_turned[n][:, a, :], q_rows[i][:, h * D : (h + 1) * D], ident_bf16[:])
 
-        def copy_queries(i, half):
-            qT[i][half] = qT_pool.tile([P, H // 2, P], BF16, name="qT_%d" % half)
-            nc.scalar.copy(out=qT[i][half][:], in_=q_turned[i, half][:])
+        def copy_queries(n, count):
+            turned = qT_pool.tile([P, count * GROUP, P], BF16, name="qT_%d" % (n % GROUPS))
+            nc.scalar.copy(out=turned[:], in_=q_turned[n][:])
+            for c in range(count):
+                qT[n + c] = turned[:, c * GROUP : (c + 1) * GROUP, :]
 
         w_grouped = keep.tile([P, PASSES * HK * D * PACK], BF16, align_bytes=64)
         w_codes = keep.tile([P, PASSES, HK * D], U32, align_bytes=64)
@@ -126,11 +140,15 @@ def tile_multiqueryattention_pa_kernel(tc, x, Wv, bv, q, k, out):
         x_grouped = {}
         v_sums = []
 
-        def group_w(g, copy):
+        def group_w(g):
             cols = slice(g * HK * D * PACK, (g + 1) * HK * D * PACK)
-            copy(
+            nc.gpsimd.tensor_scalar(
                 out=w_grouped[:, cols].rearrange("p (c t) -> p c t", t=PACK),
-                in_=w_rows[:, cols].rearrange("p (t c) -> p c t", t=PACK),
+                in0=w_rows[:, cols].rearrange("p (t c) -> p c t", t=PACK),
+                scalar1=1.0,
+                scalar2=0.0,
+                op0=ALU.mult,
+                op1=ALU.add,
             )
 
         def quantise_w():
@@ -148,10 +166,10 @@ def tile_multiqueryattention_pa_kernel(tc, x, Wv, bv, q, k, out):
                 for u in range(2):
                     nc.tensor.transpose(x_turned[g, half][:, b, u, :], words[:, u * P : (u + 1) * P], ident_f32[:])
 
-        def copy_x(g, half, copy):
+        def copy_x(g, half):
             if half == 0:
                 x_grouped[g] = x_pool.tile([P, 4 * K_PASS], BF16, align_bytes=64, name="x_grouped")
-            copy_turned(copy, x_grouped[g], half, x_turned[g, half])
+            copy_turned(x_grouped[g], half, x_turned[g, half])
 
         def quantise_x(g):
             nc.vector.quantize_mx(out=x_codes[:, g, :].bitcast(FP8X4), scales=x_scales[:, g, :], in_=x_grouped[g][:])
@@ -198,23 +216,22 @@ def tile_multiqueryattention_pa_kernel(tc, x, Wv, bv, q, k, out):
         e_codes = {}
         e_scales = {}
         o_sums = {}
+        o_rows = {}
 
         def kv_head(n):
             return (n % GROUPS) * GROUP * HK // H
 
         def score_matmul(n, a):
-            i, hq = divmod(n, GROUPS)
-            half, h = divmod(hq * GROUP + a, H // 2)
             raw_scores[n, a] = psum_scores.tile([P, T], F32, name="raw_scores")
             nc.tensor.matmul(
-                out=raw_scores[n, a][:], lhsT=qT[i][half][:, h, :], rhs=kT[kv_head(n)][:], start=True, stop=True
+                out=raw_scores[n, a][:], lhsT=qT[n][:, a, :], rhs=kT[kv_head(n)][:], start=True, stop=True
             )
 
         def upper_clip_and_max(n, a):
             b, odd = divmod(a, PAIR)
-            if a == 0:
+            if n not in row_max:
                 row_max[n] = stats.tile([P, GROUP], F32, name="row_max")
-            if odd == 0:
+            if (n, b) not in clipped:
                 clipped[n, b] = score_pool.tile([P, PAIR, T], F32, name="clipped")
             nc.vector.tensor_scalar(
                 out=clipped[n, b][:, odd, :],
@@ -232,17 +249,15 @@ def tile_multiqueryattention_pa_kernel(tc, x, Wv, bv, q, k, out):
                 out=pair, in0=pair, scalar1=RAW_CLIP, scalar2=-RAW_CLIP, op0=ALU.min, op1=ALU.max
             )
 
-        def negate_max(n, b):
-            if b == 0:
-                neg_max[n] = stats.tile([P, GROUP], F32, name="neg_max")
-            cols = slice(b * PAIR, (b + 1) * PAIR)
-            nc.scalar.mul(out=neg_max[n][:, cols], in_=row_max[n][:, cols], mul=-SCALE)
+        def negate_max(n):
+            neg_max[n] = stats.tile([P, GROUP], F32, name="neg_max")
+            nc.scalar.mul(out=neg_max[n][:], in_=row_max[n][:], mul=-SCALE)
 
         def exp(n, a):
             b, odd = divmod(a, PAIR)
-            if a == 0:
+            if n not in row_sum:
                 row_sum[n] = stats.tile([P, GROUP], F32, name="row_sum")
-            if odd == 0:
+            if (n, b) not in e_rows:
                 e_rows[n, b] = e_pool.tile([P, PAIR, T], BF16, name="e_rows")
             nc.scalar.activation(
                 out=e_rows[n, b][:, odd, :],
@@ -255,23 +270,23 @@ def tile_multiqueryattention_pa_kernel(tc, x, Wv, bv, q, k, out):
 
         def turn_e(n, a):
             b, odd = divmod(a, PAIR)
-            if odd == 0:
+            if (n, b) not in e_turned:
                 e_turned[n, b] = psum_turned.tile([P, PAIR, 2, P], F32, tag="turned", name="e_turned")
             words = e_rows[n, b][:, odd, :].bitcast(F32)
             for u in range(2):
                 nc.tensor.transpose(e_turned[n, b][:, odd, u, :], words[:, u * P : (u + 1) * P], ident_f32[:])
 
-        def copy_turned(copy, grouped, half, turned):
+        def copy_turned(grouped, half, turned, copy=nc.scalar.copy):
             words = grouped[:].bitcast(F32).rearrange("p (b r u) -> p b r u", b=4, u=2)
             copy(
                 out=words[:, 2 * half : 2 * half + 2, :, :],
                 in_=turned[:].rearrange("p b u r -> p b r u"),
             )
 
-        def copy_e(n, b, copy):
-            if b == 0:
+        def copy_e(n, b, copy=nc.scalar.copy):
+            if n not in e_grouped:
                 e_grouped[n] = e_pool.tile([P, 4 * K_PASS], BF16, align_bytes=64, name="e_grouped")
-            copy_turned(copy, e_grouped[n], b, e_turned[n, b])
+            copy_turned(e_grouped[n], b, e_turned[n, b], copy)
 
         def quantise_e(n):
             e_codes[n] = code_pool.tile([P, GROUP * P], U32, align_bytes=64, name="e_codes")
@@ -281,6 +296,7 @@ def tile_multiqueryattention_pa_kernel(tc, x, Wv, bv, q, k, out):
         def weighted_sums(n):
             j = kv_head(n)
             o_sums[n] = psum_sums.tile([P, GROUP, D], F32, tag="sums", name="o_sums")
+            o_rows[n] = out_pool.tile([P, GROUP, D], F32, name="o_rows")
             for a in range(GROUP):
                 nc.tensor.matmul_mx(
                     out=o_sums[n][:, a, :],
@@ -296,105 +312,155 @@ def tile_multiqueryattention_pa_kernel(tc, x, Wv, bv, q, k, out):
             inv_sum[n] = stats.tile([P, GROUP], F32, name="inv_sum")
             nc.vector.reciprocal(out=inv_sum[n][:], in_=row_sum[n][:])
 
-        def normalise_and_store(n, on_scalar):
-            i, hq = divmod(n, GROUPS)
-            o_rows = out_pool.tile([P, GROUP, D], F32)
-            if on_scalar:
-                for a in range(GROUP):
-                    nc.scalar.mul(out=o_rows[:, a, :], in_=o_sums[n][:, a, :], mul=inv_sum[n][:, a : a + 1])
-            else:
-                nc.vector.tensor_tensor(
-                    out=o_rows[:],
-                    in0=o_sums[n][:],
-                    in1=inv_sum[n][:].unsqueeze(2).to_broadcast([P, GROUP, D]),
-                    op=ALU.mult,
-                )
-            cols = slice(hq * GROUP * D, (hq + 1) * GROUP * D)
-            nc.sync.dma_start(out=out_view[:, i, cols], in_=o_rows[:].rearrange("p a d -> p (a d)"))
+        def divide_on_vector(n):
+            nc.vector.tensor_tensor(
+                out=o_rows[n][:, 0:VECTOR_HEADS, :],
+                in0=o_sums[n][:, 0:VECTOR_HEADS, :],
+                in1=inv_sum[n][:, 0:VECTOR_HEADS].unsqueeze(2).to_broadcast([P, VECTOR_HEADS, D]),
+                op=ALU.mult,
+            )
 
-        for half in range(2):
-            turn_queries(0, half)
-            copy_queries(0, half)
+        def divide_on_scalar_and_store(n):
+            i, hq = divmod(n, GROUPS)
+            for a in range(VECTOR_HEADS, GROUP):
+                nc.scalar.mul(out=o_rows[n][:, a, :], in_=o_sums[n][:, a, :], mul=inv_sum[n][:, a : a + 1])
+            cols = slice(hq * GROUP * D, (hq + 1) * GROUP * D)
+            nc.sync.dma_start(out=out_view[:, i, cols], in_=o_rows[n][:].rearrange("p a d -> p (a d)"))
+
+        def live(m):
+            return 0 <= m < N
+
+        turn_keys(0)
+        copy_keys(0)
+        turn_queries(0, 1)
+        copy_queries(0, 1)
         for a in range(GROUP):
             score_matmul(0, a)
 
-        attend_step = [max(n + 3, 3 + n // 2) for n in range(N)]
-        for n in range(attend_step[N - 1] + 2):
-            done = [m for m in range(N) if attend_step[m] == n - 1]
-            now = [m for m in range(N) if attend_step[m] == n]
-            i, hq = divmod(n, GROUPS)
-            turning = i + 1 < ROW_TILES and hq in (1, 2)
-            if n < N:
-                upper_clip_and_max(n, 0)
-            for m in done:
-                if m % 2 == 0:
-                    normalise_and_store(m, False)
-            if 0 <= n - 3 < N:
+        for n in range(N):
+            if live(n):
+                upper_clip_and_max(n, 1 if n > 0 else 0)
+            if live(n - 3):
                 invert_sums(n - 3)
                 quantise_e(n - 3)
-            if 0 <= n - 1 < N:
+            if live(n - 1):
                 lower_clip(n - 1, 1, nc.vector)
-            if n < N:
-                upper_clip_and_max(n, 1)
+            if live(n):
+                upper_clip_and_max(n, 0 if n > 0 else 1)
                 lower_clip(n, 0, nc.gpsimd)
-                upper_clip_and_max(n, 2)
-                upper_clip_and_max(n, 3)
-
-            m = n - 1
-            if 0 <= m < N:
-                if m == 0:
-                    negate_max(m, 0)
-                exp(m, 0)
-                turn_e(m, 0)
-            if 0 <= m - 1 < N:
-                copy_e(m - 1, 1, nc.scalar.copy)
-            if n + 1 < N:
-                score_matmul(n + 1, 0)
-            if 0 <= m < N:
-                negate_max(m, 1)
-                exp(m, 1)
-                turn_e(m, 1)
-            for d in done:
-                if not (d % 2 == 0):
-                    normalise_and_store(d, True)
-            if n + 1 < N:
-                score_matmul(n + 1, 1)
-            for d in now:
-                weighted_sums(d)
-            if turning:
-                turn_queries(i + 1, hq - 1)
-            if 0 <= m < N:
-                exp(m, 2)
-                copy_e(m, 0, nc.scalar.copy)
-                turn_e(m, 2)
-            if n + 1 < N:
-                score_matmul(n + 1, 2)
-            if n < N and n > 0:
-                negate_max(n, 0)
-            if 0 <= m < N:
-                exp(m, 3)
-                turn_e(m, 3)
-            if n + 1 < N:
-                score_matmul(n + 1, 3)
-            if turning:
-                copy_queries(i + 1, hq - 1)
-
             if n == 0:
-                for g in range(2):
-                    group_w(g, nc.vector.tensor_copy)
-                    group_w(2 + g, nc.scalar.copy)
+                turn_queries(1, 1)
+                copy_queries(1, 1)
+                turn_keys(1)
+                copy_keys(1)
+            if n == 3:
                 quantise_w()
-            if n in (0, 0 + 1):
-                for g in (2 * (n - 0), 2 * (n - 0) + 1):
-                    turn_x(g, 0)
-                    turn_x(g, 1)
-                    copy_x(g, 0, nc.vector.tensor_copy)
-                    copy_x(g, 1, nc.scalar.copy)
-                    quantise_x(g)
-            if n == 0 + 1:
+            if live(n):
+                upper_clip_and_max(n, 3 if n > 0 else 2)
+                upper_clip_and_max(n, 2 if n > 0 else 3)
+            if live(n - 5):
+                divide_on_vector(n - 5)
+            if n in (1, 2):
+                quantise_x(2 * n - 2)
+                quantise_x(2 * n - 1)
+            if n in (1, 2):
+                group_w(2 * n - 2)
+                group_w(2 * n - 1)
+
+            if live(n - 1):
+                negate_max(n - 1)
+            if live(n - 5):
+                divide_on_scalar_and_store(n - 5)
+            if live(n - 1):
+                exp(n - 1, 1)
+                exp(n - 1, 0)
+            turning = n >= 2 and (n - 2) % GROUPS < 2 and live(n - n % GROUPS + GROUPS)
+            half = n - n % GROUPS + GROUPS + 2 * ((n - 2) % GROUPS)
+            if turning:
+                turn_queries(half, 2)
+            if live(n - 2):
+                turn_e(n - 2, 3)
+                turn_e(n - 2, 2)
+            if n == 0:
+                turn_x(0, 0)
+                copy_x(0, 0)
+            if live(n + 1):
+                score_matmul(n + 1, 0)
+                score_matmul(n + 1, 1)
+            if n == 0:
+                turn_x(0, 1)
+                copy_x(0, 1)
+                turn_x(1, 0)
+                copy_x(1, 0)
+            if n == 1:
+                for half_x in range(2):
+                    turn_x(3, half_x)
+                    copy_x(3, half_x)
+            if live(n - 2):
+                copy_e(n - 2, 1)
+                copy_e(n - 2, 0)
+            if live(n - 4):
+                weighted_sums(n - 4)
+            if live(n - 1):
+                turn_e(n - 1, 1)
+                turn_e(n - 1, 0)
+                exp(n - 1, 3)
+                exp(n - 1, 2)
+            if turning:
+                copy_queries(half, 2)
+            if n == 3:
                 value_matmuls(0)
                 value_matmuls(1)
-                add_bias(0)
-                quantise_v(0)
-                add_bias(1)
-                quantise_v(1)
+                for j in range(HK):
+                    add_bias(j)
+                for j in range(HK):
+                    quantise_v(j)
+            if live(n + 1):
+                score_matmul(n + 1, 2)
+                score_matmul(n + 1, 3)
+            if n == 0:
+                turn_queries(2, 2)
+                copy_queries(2, 2)
+                turn_x(1, 1)
+                copy_x(1, 1)
+                for half_x in range(2):
+                    turn_x(2, half_x)
+                    copy_x(2, half_x)
+
+        last = N - 1
+        lower_clip(last, 1, nc.vector)
+        turn_e(last - 1, 3)
+        turn_e(last - 1, 2)
+        copy_e(last - 1, 1, nc.vector.tensor_copy)
+        copy_e(last - 1, 0, nc.vector.tensor_copy)
+        negate_max(last)
+        invert_sums(last - 2)
+        quantise_e(last - 2)
+        weighted_sums(last - 3)
+        exp(last, 1)
+        exp(last, 0)
+        turn_e(last, 1)
+        turn_e(last, 0)
+        divide_on_vector(last - 4)
+        divide_on_scalar_and_store(last - 4)
+        exp(last, 3)
+        exp(last, 2)
+        turn_e(last, 3)
+        turn_e(last, 2)
+        invert_sums(last - 1)
+        quantise_e(last - 1)
+        weighted_sums(last - 2)
+        copy_e(last, 0, nc.vector.tensor_copy)
+        divide_on_vector(last - 3)
+        divide_on_scalar_and_store(last - 3)
+        weighted_sums(last - 1)
+        copy_e(last, 1, nc.scalar.copy)
+        invert_sums(last)
+        divide_on_vector(last - 2)
+        divide_on_scalar_and_store(last - 2)
+        quantise_e(last)
+        divide_on_vector(last - 1)
+        divide_on_scalar_and_store(last - 1)
+        weighted_sums(last)
+        divide_on_vector(last)
+        divide_on_scalar_and_store(last)

@@ -74,12 +74,12 @@ def tile_multiqueryattention_pa_kernel(tc, x, Wv, bv, q, k, out):
             nc.sync.dma_start(out=x_rows[half][:], in_=x_view[:, :, half * C // 2 : (half + 1) * C // 2])
             if half == 0:
                 load_queries(0, 1, 2)
+        load_queries(0, 2, GROUPS)
         w_rows = keep.tile([P, C * HK * D // P], BF16)
         nc.sync.dma_start(
             out=w_rows[:].rearrange("p (s f) -> p s f", s=2 * PASSES),
             in_=Wv.rearrange("(s p e) c -> p s (e c)", p=P, e=2),
         )
-        load_queries(0, 2, GROUPS)
         bias_rows = keep.tile([P, HK * D], BF16)
         nc.sync.dma_start(out=bias_rows[:], in_=bv.partition_broadcast(P))
         for i in range(1, ROW_TILES):
@@ -142,13 +142,9 @@ def tile_multiqueryattention_pa_kernel(tc, x, Wv, bv, q, k, out):
 
         def group_w(g):
             cols = slice(g * HK * D * PACK, (g + 1) * HK * D * PACK)
-            nc.gpsimd.tensor_scalar(
+            nc.vector.tensor_copy(
                 out=w_grouped[:, cols].rearrange("p (c t) -> p c t", t=PACK),
-                in0=w_rows[:, cols].rearrange("p (t c) -> p c t", t=PACK),
-                scalar1=1.0,
-                scalar2=0.0,
-                op0=ALU.mult,
-                op1=ALU.add,
+                in_=w_rows[:, cols].rearrange("p (t c) -> p c t", t=PACK),
             )
 
         def quantise_w():
@@ -312,20 +308,28 @@ def tile_multiqueryattention_pa_kernel(tc, x, Wv, bv, q, k, out):
             inv_sum[n] = stats.tile([P, GROUP], F32, name="inv_sum")
             nc.vector.reciprocal(out=inv_sum[n][:], in_=row_sum[n][:])
 
-        def divide_on_vector(n):
-            nc.vector.tensor_tensor(
-                out=o_rows[n][:, 0:VECTOR_HEADS, :],
-                in0=o_sums[n][:, 0:VECTOR_HEADS, :],
-                in1=inv_sum[n][:, 0:VECTOR_HEADS].unsqueeze(2).to_broadcast([P, VECTOR_HEADS, D]),
-                op=ALU.mult,
-            )
-
-        def divide_on_scalar_and_store(n):
+        def divide_and_store(n, on_scalar):
             i, hq = divmod(n, GROUPS)
-            for a in range(VECTOR_HEADS, GROUP):
-                nc.scalar.mul(out=o_rows[n][:, a, :], in_=o_sums[n][:, a, :], mul=inv_sum[n][:, a : a + 1])
+            if on_scalar:
+                for a in range(GROUP):
+                    nc.scalar.mul(out=o_rows[n][:, a, :], in_=o_sums[n][:, a, :], mul=inv_sum[n][:, a : a + 1])
+            else:
+                nc.vector.tensor_tensor(
+                    out=o_rows[n][:],
+                    in0=o_sums[n][:],
+                    in1=inv_sum[n][:].unsqueeze(2).to_broadcast([P, GROUP, D]),
+                    op=ALU.mult,
+                )
             cols = slice(hq * GROUP * D, (hq + 1) * GROUP * D)
             nc.sync.dma_start(out=out_view[:, i, cols], in_=o_rows[n][:].rearrange("p a d -> p (a d)"))
+
+        def divide_V(n):
+            if not (n % 2 == 1):
+                divide_and_store(n, False)
+
+        def divide_S(n):
+            if n % 2 == 1:
+                divide_and_store(n, True)
 
         def live(m):
             return 0 <= m < N
@@ -345,6 +349,14 @@ def tile_multiqueryattention_pa_kernel(tc, x, Wv, bv, q, k, out):
                 quantise_e(n - 3)
             if live(n - 1):
                 lower_clip(n - 1, 1, nc.vector)
+            if n == 2:
+                quantise_x(0)
+                quantise_x(1)
+                for g in range(PASSES):
+                    group_w(g)
+            if n == 3:
+                quantise_x(2)
+                quantise_x(3)
             if live(n):
                 upper_clip_and_max(n, 0 if n > 0 else 1)
                 lower_clip(n, 0, nc.gpsimd)
@@ -359,18 +371,12 @@ def tile_multiqueryattention_pa_kernel(tc, x, Wv, bv, q, k, out):
                 upper_clip_and_max(n, 3 if n > 0 else 2)
                 upper_clip_and_max(n, 2 if n > 0 else 3)
             if live(n - 5):
-                divide_on_vector(n - 5)
-            if n in (1, 2):
-                quantise_x(2 * n - 2)
-                quantise_x(2 * n - 1)
-            if n in (1, 2):
-                group_w(2 * n - 2)
-                group_w(2 * n - 1)
+                divide_V(n - 5)
 
             if live(n - 1):
                 negate_max(n - 1)
             if live(n - 5):
-                divide_on_scalar_and_store(n - 5)
+                divide_S(n - 5)
             if live(n - 1):
                 exp(n - 1, 1)
                 exp(n - 1, 0)
@@ -394,8 +400,8 @@ def tile_multiqueryattention_pa_kernel(tc, x, Wv, bv, q, k, out):
                 copy_x(1, 0)
             if n == 1:
                 for half_x in range(2):
-                    turn_x(3, half_x)
-                    copy_x(3, half_x)
+                    turn_x(2, half_x)
+                    copy_x(2, half_x)
             if live(n - 2):
                 copy_e(n - 2, 1)
                 copy_e(n - 2, 0)
@@ -406,6 +412,10 @@ def tile_multiqueryattention_pa_kernel(tc, x, Wv, bv, q, k, out):
                 turn_e(n - 1, 0)
                 exp(n - 1, 3)
                 exp(n - 1, 2)
+            if n == 1:
+                for half_x in range(2):
+                    turn_x(3, half_x)
+                    copy_x(3, half_x)
             if turning:
                 copy_queries(half, 2)
             if n == 3:
@@ -423,9 +433,6 @@ def tile_multiqueryattention_pa_kernel(tc, x, Wv, bv, q, k, out):
                 copy_queries(2, 2)
                 turn_x(1, 1)
                 copy_x(1, 1)
-                for half_x in range(2):
-                    turn_x(2, half_x)
-                    copy_x(2, half_x)
 
         last = N - 1
         lower_clip(last, 1, nc.vector)
@@ -441,8 +448,8 @@ def tile_multiqueryattention_pa_kernel(tc, x, Wv, bv, q, k, out):
         exp(last, 0)
         turn_e(last, 1)
         turn_e(last, 0)
-        divide_on_vector(last - 4)
-        divide_on_scalar_and_store(last - 4)
+        divide_V(last - 4)
+        divide_S(last - 4)
         exp(last, 3)
         exp(last, 2)
         turn_e(last, 3)
@@ -451,16 +458,16 @@ def tile_multiqueryattention_pa_kernel(tc, x, Wv, bv, q, k, out):
         quantise_e(last - 1)
         weighted_sums(last - 2)
         copy_e(last, 0, nc.vector.tensor_copy)
-        divide_on_vector(last - 3)
-        divide_on_scalar_and_store(last - 3)
+        divide_V(last - 3)
+        divide_S(last - 3)
         weighted_sums(last - 1)
         copy_e(last, 1, nc.scalar.copy)
         invert_sums(last)
-        divide_on_vector(last - 2)
-        divide_on_scalar_and_store(last - 2)
+        divide_V(last - 2)
+        divide_S(last - 2)
         quantise_e(last)
-        divide_on_vector(last - 1)
-        divide_on_scalar_and_store(last - 1)
+        divide_V(last - 1)
+        divide_S(last - 1)
         weighted_sums(last)
-        divide_on_vector(last)
-        divide_on_scalar_and_store(last)
+        divide_V(last)
+        divide_S(last)

@@ -205,6 +205,7 @@ def tile_multiqueryattention_pa_kernel(tc, x, Wv, bv, q, k, out):
         row_max = {}
         neg_max = {}
         row_sum = {}
+        row_sums = {}
         inv_sum = {}
         e_rows = {}
         e_turned = {}
@@ -251,8 +252,11 @@ def tile_multiqueryattention_pa_kernel(tc, x, Wv, bv, q, k, out):
 
         def exp(n, a):
             b, odd = divmod(a, PAIR)
-            if n not in row_sum:
-                row_sum[n] = stats.tile([P, GROUP], F32, name="row_sum")
+            if n % 2 == 0 and n not in row_sum:
+                both = stats.tile([P, 2 * GROUP], F32, name="row_sum")
+                row_sum[n] = both[:, 0:GROUP]
+                row_sum[n + 1] = both[:, GROUP : 2 * GROUP]
+                row_sums[n] = both
             if (n, b) not in e_rows:
                 e_rows[n, b] = e_pool.tile([P, PAIR, T], BF16, name="e_rows")
             nc.scalar.activation(
@@ -304,9 +308,49 @@ def tile_multiqueryattention_pa_kernel(tc, x, Wv, bv, q, k, out):
                     stop=True,
                 )
 
+        def quantise_pair(n, b):
+            if b == 0:
+                e_codes[n] = code_pool.tile([P, GROUP * P], U32, align_bytes=64, name="e_codes")
+                e_scales[n] = code_pool.tile([P, GROUP * P], U8, align_bytes=64, name="e_scales")
+            cols = slice(b * PAIR * P, (b + 1) * PAIR * P)
+            nc.vector.quantize_mx(
+                out=e_codes[n][:, cols].bitcast(FP8X4),
+                scales=e_scales[n][:, cols],
+                in_=e_grouped[n][:, b * PAIR * K_PASS : (b + 1) * PAIR * K_PASS],
+            )
+
+        def weighted_sums_pair(n, b):
+            j = kv_head(n)
+            o_sums[n, b] = psum_scores.tile([P, PAIR, D], F32, tag="raw_scores", name="o_sums_pair")
+            o_rows[n, b] = out_pool.tile([P, PAIR, D], F32, name="o_rows_pair")
+            for c in range(PAIR):
+                a = b * PAIR + c
+                nc.tensor.matmul_mx(
+                    out=o_sums[n, b][:, c, :],
+                    lhsT=e_codes[n][:, a * P : (a + 1) * P].bitcast(FP8X4),
+                    lhsT_scale=e_scales[n][:, a * P : (a + 1) * P],
+                    rhs=v_codes[j][:].bitcast(FP8X4),
+                    rhs_scale=v_scales[j][:],
+                    start=True,
+                    stop=True,
+                )
+
+        def divide_pair(n, b):
+            i, hq = divmod(n, GROUPS)
+            nc.vector.tensor_tensor(
+                out=o_rows[n, b][:],
+                in0=o_sums[n, b][:],
+                in1=inv_sum[n][:, b * PAIR : (b + 1) * PAIR].unsqueeze(2).to_broadcast([P, PAIR, D]),
+                op=ALU.mult,
+            )
+            h0 = hq * GROUP + b * PAIR
+            nc.sync.dma_start(out=out_view[:, i, h0 * D : (h0 + PAIR) * D], in_=o_rows[n, b][:].rearrange("p a d -> p (a d)"))
+
         def invert_sums(n):
-            inv_sum[n] = stats.tile([P, GROUP], F32, name="inv_sum")
-            nc.vector.reciprocal(out=inv_sum[n][:], in_=row_sum[n][:])
+            both = stats.tile([P, 2 * GROUP], F32, name="inv_sum")
+            nc.vector.reciprocal(out=both[:], in_=row_sums[n][:])
+            inv_sum[n] = both[:, 0:GROUP]
+            inv_sum[n + 1] = both[:, GROUP : 2 * GROUP]
 
         def divide_and_store(n, on_scalar):
             i, hq = divmod(n, GROUPS)
@@ -317,18 +361,18 @@ def tile_multiqueryattention_pa_kernel(tc, x, Wv, bv, q, k, out):
                 nc.vector.tensor_tensor(
                     out=o_rows[n][:],
                     in0=o_sums[n][:],
-                    in1=inv_sum[n][:].unsqueeze(2).to_broadcast([P, GROUP, D]),
+                    in1=inv_sum[n].unsqueeze(2).to_broadcast([P, GROUP, D]),
                     op=ALU.mult,
                 )
             cols = slice(hq * GROUP * D, (hq + 1) * GROUP * D)
             nc.sync.dma_start(out=out_view[:, i, cols], in_=o_rows[n][:].rearrange("p a d -> p (a d)"))
 
         def divide_V(n):
-            if not (n % 2 == 1):
+            if not (n % 4 == 1 or n >= 12):
                 divide_and_store(n, False)
 
         def divide_S(n):
-            if n % 2 == 1:
+            if n % 4 == 1 or n >= 12:
                 divide_and_store(n, True)
 
         def live(m):
@@ -345,8 +389,9 @@ def tile_multiqueryattention_pa_kernel(tc, x, Wv, bv, q, k, out):
             if live(n):
                 upper_clip_and_max(n, 1 if n > 0 else 0)
             if live(n - 3):
-                invert_sums(n - 3)
                 quantise_e(n - 3)
+            if live(n - 4) and n % 2 == 0:
+                invert_sums(n - 4)
             if live(n - 1):
                 lower_clip(n - 1, 1, nc.vector)
             if n == 2:
@@ -438,10 +483,10 @@ def tile_multiqueryattention_pa_kernel(tc, x, Wv, bv, q, k, out):
         lower_clip(last, 1, nc.vector)
         turn_e(last - 1, 3)
         turn_e(last - 1, 2)
-        copy_e(last - 1, 1, nc.vector.tensor_copy)
         copy_e(last - 1, 0, nc.vector.tensor_copy)
+        copy_e(last - 1, 1, nc.vector.tensor_copy)
         negate_max(last)
-        invert_sums(last - 2)
+        invert_sums(last - 3)
         quantise_e(last - 2)
         weighted_sums(last - 3)
         exp(last, 1)
@@ -449,25 +494,26 @@ def tile_multiqueryattention_pa_kernel(tc, x, Wv, bv, q, k, out):
         turn_e(last, 1)
         turn_e(last, 0)
         divide_V(last - 4)
-        divide_S(last - 4)
         exp(last, 3)
         exp(last, 2)
         turn_e(last, 3)
         turn_e(last, 2)
-        invert_sums(last - 1)
+        divide_S(last - 4)
         quantise_e(last - 1)
         weighted_sums(last - 2)
         copy_e(last, 0, nc.vector.tensor_copy)
+        quantise_pair(last, 0)
+        weighted_sums_pair(last, 0)
         divide_V(last - 3)
         divide_S(last - 3)
+        copy_e(last, 1, nc.vector.tensor_copy)
         weighted_sums(last - 1)
-        copy_e(last, 1, nc.scalar.copy)
-        invert_sums(last)
-        divide_V(last - 2)
+        invert_sums(last - 1)
+        quantise_pair(last, 1)
+        weighted_sums_pair(last, 1)
         divide_S(last - 2)
-        quantise_e(last)
-        divide_V(last - 1)
+        divide_V(last - 2)
+        divide_pair(last, 0)
         divide_S(last - 1)
-        weighted_sums(last)
-        divide_V(last)
-        divide_S(last)
+        divide_V(last - 1)
+        divide_pair(last, 1)

@@ -26,7 +26,7 @@ PASSES = C // K_PASS
 PAIR = 2
 GROUP = 4
 GROUPS = H // GROUP
-VECTOR_HEADS = 3
+N = ROW_TILES * GROUPS
 
 SCALE = 1.0 / math.sqrt(D)
 CLIP = 100.0
@@ -46,9 +46,9 @@ def tile_multiqueryattention_pa_kernel(tc, x, Wv, bv, q, k, out):
         x_pool = ctx.enter_context(tc.tile_pool(name="x_pool", bufs=PASSES))
         e_pool = ctx.enter_context(tc.tile_pool(name="e_pool", bufs=6))
         code_pool = ctx.enter_context(tc.tile_pool(name="code_pool", bufs=5))
-        out_pool = ctx.enter_context(tc.tile_pool(name="out_pool", bufs=4))
+        out_pool = ctx.enter_context(tc.tile_pool(name="out_pool", bufs=8))
         stats = ctx.enter_context(tc.tile_pool(name="stats", bufs=16))
-        psum_scores = ctx.enter_context(tc.psum_pool(name="psum_scores", bufs=2 * PAIR))
+        psum_scores = ctx.enter_context(tc.psum_pool(name="psum_scores", bufs=GROUP))
         psum_turned = ctx.enter_context(tc.psum_pool(name="psum_turned", bufs=2))
         psum_sums = ctx.enter_context(tc.psum_pool(name="psum_sums", bufs=2))
 
@@ -68,13 +68,11 @@ def tile_multiqueryattention_pa_kernel(tc, x, Wv, bv, q, k, out):
             nc.sync.dma_start(out=q_rows[i][:, cols], in_=q_view[:, i, cols])
 
         load_queries(0, 0, 1)
+        load_queries(0, 1, GROUPS)
         x_rows = []
         for half in range(2):
             x_rows.append(keep.tile([P, ROW_TILES, C // 2], BF16, name="x_rows_%d" % half))
             nc.sync.dma_start(out=x_rows[half][:], in_=x_view[:, :, half * C // 2 : (half + 1) * C // 2])
-            if half == 0:
-                load_queries(0, 1, 2)
-        load_queries(0, 2, GROUPS)
         w_rows = keep.tile([P, C * HK * D // P], BF16)
         nc.sync.dma_start(
             out=w_rows[:].rearrange("p (s f) -> p s f", s=2 * PASSES),
@@ -102,15 +100,15 @@ def tile_multiqueryattention_pa_kernel(tc, x, Wv, bv, q, k, out):
             for i in range(ROW_TILES):
                 nc.tensor.transpose(k_turned[j][:, i, :], k_rows[:, i, j * D : (j + 1) * D], ident_bf16[:])
 
-        def copy_keys(j):
+        def copy_keys(j, copy):
             kT[j] = keep.tile([P, T], BF16, name="kT_%d" % j)
-            nc.vector.tensor_copy(
+            copy(
                 out=kT[j][:].rearrange("p (u r e) -> p u r e", u=2, e=2),
                 in_=k_turned[j][:].rearrange("p (u e) r -> p u r e", u=2),
             )
 
-        qT = {}
-        q_turned = {}
+        qT = [None] * N
+        q_turned = [None] * N
 
         def turn_queries(n, count):
             i, hq = divmod(n, GROUPS)
@@ -125,6 +123,18 @@ def tile_multiqueryattention_pa_kernel(tc, x, Wv, bv, q, k, out):
             for c in range(count):
                 qT[n + c] = turned[:, c * GROUP : (c + 1) * GROUP, :]
 
+        def turn_block(turned, b, block):
+            words = block.bitcast(F32)
+            for u in range(2):
+                nc.tensor.transpose(turned[:, b, u, :], words[:, u * P : (u + 1) * P], ident_f32[:])
+
+        def copy_turned(grouped, half, turned, copy):
+            words = grouped[:].bitcast(F32).rearrange("p (b r u) -> p b r u", b=4, u=2)
+            copy(
+                out=words[:, 2 * half : 2 * half + 2, :, :],
+                in_=turned[:].rearrange("p b u r -> p b r u"),
+            )
+
         w_grouped = keep.tile([P, PASSES * HK * D * PACK], BF16, align_bytes=64)
         w_codes = keep.tile([P, PASSES, HK * D], U32, align_bytes=64)
         w_scales = keep.tile([P, PASSES, HK * D], U8, align_bytes=64)
@@ -136,8 +146,7 @@ def tile_multiqueryattention_pa_kernel(tc, x, Wv, bv, q, k, out):
         for j in range(HK):
             v_codes.append(keep.tile([P, D], U32, align_bytes=64, name="v_codes_%d" % j))
             v_scales.append(keep.tile([P, D], U8, align_bytes=64, name="v_scales_%d" % j))
-        x_turned = {}
-        x_grouped = {}
+        x_grouped = [None] * PASSES
         v_sums = []
 
         def group_w(g):
@@ -154,18 +163,14 @@ def tile_multiqueryattention_pa_kernel(tc, x, Wv, bv, q, k, out):
                 in_=w_grouped[:],
             )
 
-        def turn_x(g, half):
-            x_turned[g, half] = psum_sums.tile([P, 2, 2, P], F32, tag="sums", name="x_turned")
-            for b in range(2):
-                part, k0 = divmod(g * K_PASS, C // 2)
-                words = x_rows[part][:, 2 * half + b, k0 : k0 + K_PASS].bitcast(F32)
-                for u in range(2):
-                    nc.tensor.transpose(x_turned[g, half][:, b, u, :], words[:, u * P : (u + 1) * P], ident_f32[:])
-
-        def copy_x(g, half):
+        def turn_and_copy_x(g, half):
             if half == 0:
                 x_grouped[g] = x_pool.tile([P, 4 * K_PASS], BF16, align_bytes=64, name="x_grouped")
-            copy_turned(x_grouped[g], half, x_turned[g, half])
+            x_turned = psum_sums.tile([P, 2, 2, P], F32, tag="sums", name="x_turned")
+            part, k0 = divmod(g * K_PASS, C // 2)
+            for b in range(2):
+                turn_block(x_turned, b, x_rows[part][:, 2 * half + b, k0 : k0 + K_PASS])
+            copy_turned(x_grouped[g], half, x_turned, nc.scalar.copy)
 
         def quantise_x(g):
             nc.vector.quantize_mx(out=x_codes[:, g, :].bitcast(FP8X4), scales=x_scales[:, g, :], in_=x_grouped[g][:])
@@ -199,39 +204,36 @@ def tile_multiqueryattention_pa_kernel(tc, x, Wv, bv, q, k, out):
                 in_=v_grouped[:, j, :, :].rearrange("p c t -> p (c t)"),
             )
 
-        N = ROW_TILES * GROUPS
         raw_scores = {}
         clipped = {}
-        row_max = {}
-        neg_max = {}
-        row_sum = {}
-        row_sums = {}
-        inv_sum = {}
+        row_max = [None] * N
+        neg_max = [None] * N
+        row_sums = [None] * N
+        inv_sums = [None] * N
         e_rows = {}
         e_turned = {}
-        e_grouped = {}
-        e_codes = {}
-        e_scales = {}
+        e_grouped = [None] * N
+        e_codes = [None] * N
+        e_scales = [None] * N
         o_sums = {}
-        o_rows = {}
 
         def kv_head(n):
             return (n % GROUPS) * GROUP * HK // H
 
         def score_matmul(n, a):
-            raw_scores[n, a] = psum_scores.tile([P, T], F32, name="raw_scores")
+            raw_scores[n, a] = psum_scores.tile([P, T], F32, tag="scores", name="raw_scores")
             nc.tensor.matmul(
                 out=raw_scores[n, a][:], lhsT=qT[n][:, a, :], rhs=kT[kv_head(n)][:], start=True, stop=True
             )
 
         def upper_clip_and_max(n, a):
-            b, odd = divmod(a, PAIR)
-            if n not in row_max:
+            b, c = divmod(a, PAIR)
+            if row_max[n] is None:
                 row_max[n] = stats.tile([P, GROUP], F32, name="row_max")
             if (n, b) not in clipped:
                 clipped[n, b] = score_pool.tile([P, PAIR, T], F32, name="clipped")
             nc.vector.tensor_scalar(
-                out=clipped[n, b][:, odd, :],
+                out=clipped[n, b][:, c, :],
                 in0=raw_scores[n, a][:],
                 scalar1=RAW_CLIP,
                 scalar2=-RAW_CLIP,
@@ -250,83 +252,53 @@ def tile_multiqueryattention_pa_kernel(tc, x, Wv, bv, q, k, out):
             neg_max[n] = stats.tile([P, GROUP], F32, name="neg_max")
             nc.scalar.mul(out=neg_max[n][:], in_=row_max[n][:], mul=-SCALE)
 
+        def sum_column(n, a):
+            return (n % 2) * GROUP + a
+
         def exp(n, a):
-            b, odd = divmod(a, PAIR)
-            if n % 2 == 0 and n not in row_sum:
-                both = stats.tile([P, 2 * GROUP], F32, name="row_sum")
-                row_sum[n] = both[:, 0:GROUP]
-                row_sum[n + 1] = both[:, GROUP : 2 * GROUP]
-                row_sums[n] = both
+            b, c = divmod(a, PAIR)
+            if row_sums[n] is None:
+                row_sums[n] = stats.tile([P, 2 * GROUP], F32, name="row_sums")
+                row_sums[n + 1] = row_sums[n]
             if (n, b) not in e_rows:
                 e_rows[n, b] = e_pool.tile([P, PAIR, T], BF16, name="e_rows")
+            col = sum_column(n, a)
             nc.scalar.activation(
-                out=e_rows[n, b][:, odd, :],
-                in_=clipped[n, b][:, odd, :],
+                out=e_rows[n, b][:, c, :],
+                in_=clipped[n, b][:, c, :],
                 func=ACT.Exp,
                 bias=neg_max[n][:, a : a + 1],
                 scale=SCALE,
-                accum_out=row_sum[n][:, a : a + 1],
+                accum_out=row_sums[n][:, col : col + 1],
             )
 
         def turn_e(n, a):
-            b, odd = divmod(a, PAIR)
+            b, c = divmod(a, PAIR)
             if (n, b) not in e_turned:
                 e_turned[n, b] = psum_turned.tile([P, PAIR, 2, P], F32, tag="turned", name="e_turned")
-            words = e_rows[n, b][:, odd, :].bitcast(F32)
-            for u in range(2):
-                nc.tensor.transpose(e_turned[n, b][:, odd, u, :], words[:, u * P : (u + 1) * P], ident_f32[:])
+            turn_block(e_turned[n, b], c, e_rows[n, b][:, c, :])
 
-        def copy_turned(grouped, half, turned, copy=nc.scalar.copy):
-            words = grouped[:].bitcast(F32).rearrange("p (b r u) -> p b r u", b=4, u=2)
-            copy(
-                out=words[:, 2 * half : 2 * half + 2, :, :],
-                in_=turned[:].rearrange("p b u r -> p b r u"),
-            )
-
-        def copy_e(n, b, copy=nc.scalar.copy):
-            if n not in e_grouped:
+        def copy_e(n, b, copy):
+            if e_grouped[n] is None:
                 e_grouped[n] = e_pool.tile([P, 4 * K_PASS], BF16, align_bytes=64, name="e_grouped")
             copy_turned(e_grouped[n], b, e_turned[n, b], copy)
 
-        def quantise_e(n):
-            e_codes[n] = code_pool.tile([P, GROUP * P], U32, align_bytes=64, name="e_codes")
-            e_scales[n] = code_pool.tile([P, GROUP * P], U8, align_bytes=64, name="e_scales")
-            nc.vector.quantize_mx(out=e_codes[n][:].bitcast(FP8X4), scales=e_scales[n][:], in_=e_grouped[n][:])
-
-        def weighted_sums(n):
-            j = kv_head(n)
-            o_sums[n] = psum_sums.tile([P, GROUP, D], F32, tag="sums", name="o_sums")
-            o_rows[n] = out_pool.tile([P, GROUP, D], F32, name="o_rows")
-            for a in range(GROUP):
-                nc.tensor.matmul_mx(
-                    out=o_sums[n][:, a, :],
-                    lhsT=e_codes[n][:, a * P : (a + 1) * P].bitcast(FP8X4),
-                    lhsT_scale=e_scales[n][:, a * P : (a + 1) * P],
-                    rhs=v_codes[j][:].bitcast(FP8X4),
-                    rhs_scale=v_scales[j][:],
-                    start=True,
-                    stop=True,
-                )
-
-        def quantise_pair(n, b):
-            if b == 0:
+        def quantise_e(n, first, end):
+            if e_codes[n] is None:
                 e_codes[n] = code_pool.tile([P, GROUP * P], U32, align_bytes=64, name="e_codes")
                 e_scales[n] = code_pool.tile([P, GROUP * P], U8, align_bytes=64, name="e_scales")
-            cols = slice(b * PAIR * P, (b + 1) * PAIR * P)
             nc.vector.quantize_mx(
-                out=e_codes[n][:, cols].bitcast(FP8X4),
-                scales=e_scales[n][:, cols],
-                in_=e_grouped[n][:, b * PAIR * K_PASS : (b + 1) * PAIR * K_PASS],
+                out=e_codes[n][:, first * P : end * P].bitcast(FP8X4),
+                scales=e_scales[n][:, first * P : end * P],
+                in_=e_grouped[n][:, first * K_PASS : end * K_PASS],
             )
 
-        def weighted_sums_pair(n, b):
+        def weighted_sums(n, first, end, sums):
             j = kv_head(n)
-            o_sums[n, b] = psum_scores.tile([P, PAIR, D], F32, tag="raw_scores", name="o_sums_pair")
-            o_rows[n, b] = out_pool.tile([P, PAIR, D], F32, name="o_rows_pair")
-            for c in range(PAIR):
-                a = b * PAIR + c
+            o_sums[n, first] = sums
+            for a in range(first, end):
                 nc.tensor.matmul_mx(
-                    out=o_sums[n, b][:, c, :],
+                    out=sums[:, a - first, :],
                     lhsT=e_codes[n][:, a * P : (a + 1) * P].bitcast(FP8X4),
                     lhsT_scale=e_scales[n][:, a * P : (a + 1) * P],
                     rhs=v_codes[j][:].bitcast(FP8X4),
@@ -335,64 +307,52 @@ def tile_multiqueryattention_pa_kernel(tc, x, Wv, bv, q, k, out):
                     stop=True,
                 )
 
-        def divide_pair(n, b):
-            i, hq = divmod(n, GROUPS)
-            nc.vector.tensor_tensor(
-                out=o_rows[n, b][:],
-                in0=o_sums[n, b][:],
-                in1=inv_sum[n][:, b * PAIR : (b + 1) * PAIR].unsqueeze(2).to_broadcast([P, PAIR, D]),
-                op=ALU.mult,
-            )
-            h0 = hq * GROUP + b * PAIR
-            nc.sync.dma_start(out=out_view[:, i, h0 * D : (h0 + PAIR) * D], in_=o_rows[n, b][:].rearrange("p a d -> p (a d)"))
+        def group_sums(n):
+            sums = psum_sums.tile([P, GROUP, D], F32, tag="sums", name="o_sums")
+            weighted_sums(n, 0, GROUP, sums)
 
         def invert_sums(n):
-            both = stats.tile([P, 2 * GROUP], F32, name="inv_sum")
-            nc.vector.reciprocal(out=both[:], in_=row_sums[n][:])
-            inv_sum[n] = both[:, 0:GROUP]
-            inv_sum[n + 1] = both[:, GROUP : 2 * GROUP]
+            inv_sums[n] = stats.tile([P, 2 * GROUP], F32, name="inv_sums")
+            inv_sums[n + 1] = inv_sums[n]
+            nc.vector.reciprocal(out=inv_sums[n][:], in_=row_sums[n][:])
 
-        def divide_and_store(n, on_scalar):
+        def divide_and_store(n, first, end, on_scalar):
             i, hq = divmod(n, GROUPS)
+            sums = o_sums[n, first]
+            o_rows = out_pool.tile([P, end - first, D], F32, name="o_rows")
+            col = sum_column(n, first)
             if on_scalar:
-                for a in range(GROUP):
-                    nc.scalar.mul(out=o_rows[n][:, a, :], in_=o_sums[n][:, a, :], mul=inv_sum[n][:, a : a + 1])
+                for a in range(end - first):
+                    nc.scalar.mul(
+                        out=o_rows[:, a, :], in_=sums[:, a, :], mul=inv_sums[n][:, col + a : col + a + 1]
+                    )
             else:
                 nc.vector.tensor_tensor(
-                    out=o_rows[n][:],
-                    in0=o_sums[n][:],
-                    in1=inv_sum[n].unsqueeze(2).to_broadcast([P, GROUP, D]),
+                    out=o_rows[:],
+                    in0=sums[:],
+                    in1=inv_sums[n][:, col : col + end - first].unsqueeze(2).to_broadcast([P, end - first, D]),
                     op=ALU.mult,
                 )
-            cols = slice(hq * GROUP * D, (hq + 1) * GROUP * D)
-            nc.sync.dma_start(out=out_view[:, i, cols], in_=o_rows[n][:].rearrange("p a d -> p (a d)"))
+            cols = slice((hq * GROUP + first) * D, (hq * GROUP + end) * D)
+            nc.sync.dma_start(out=out_view[:, i, cols], in_=o_rows[:].rearrange("p a d -> p (a d)"))
 
-        def divide_V(n):
-            if not (n % 4 == 1 or n >= 12):
-                divide_and_store(n, False)
-
-        def divide_S(n):
-            if n % 4 == 1 or n >= 12:
-                divide_and_store(n, True)
-
-        def live(m):
-            return 0 <= m < N
+        def scalar_divides(n):
+            return n % 4 == 1
 
         turn_keys(0)
-        copy_keys(0)
+        copy_keys(0, nc.vector.tensor_copy)
         turn_queries(0, 1)
         copy_queries(0, 1)
         for a in range(GROUP):
             score_matmul(0, a)
 
         for n in range(N):
-            if live(n):
-                upper_clip_and_max(n, 1 if n > 0 else 0)
-            if live(n - 3):
-                quantise_e(n - 3)
-            if live(n - 4) and n % 2 == 0:
+            upper_clip_and_max(n, 1 if n > 0 else 0)
+            if n >= 3:
+                quantise_e(n - 3, 0, GROUP)
+            if n >= 4 and n % 2 == 0:
                 invert_sums(n - 4)
-            if live(n - 1):
+            if n >= 1:
                 lower_clip(n - 1, 1, nc.vector)
             if n == 2:
                 quantise_x(0)
@@ -402,84 +362,82 @@ def tile_multiqueryattention_pa_kernel(tc, x, Wv, bv, q, k, out):
             if n == 3:
                 quantise_x(2)
                 quantise_x(3)
-            if live(n):
-                upper_clip_and_max(n, 0 if n > 0 else 1)
-                lower_clip(n, 0, nc.gpsimd)
+            if n == 4:
+                for j in range(HK):
+                    add_bias(j)
+                for j in range(HK):
+                    quantise_v(j)
+            upper_clip_and_max(n, 0 if n > 0 else 1)
+            lower_clip(n, 0, nc.gpsimd)
             if n == 0:
                 turn_queries(1, 1)
                 copy_queries(1, 1)
                 turn_keys(1)
-                copy_keys(1)
+                copy_keys(1, nc.scalar.copy)
             if n == 3:
                 quantise_w()
-            if live(n):
-                upper_clip_and_max(n, 3 if n > 0 else 2)
-                upper_clip_and_max(n, 2 if n > 0 else 3)
-            if live(n - 5):
-                divide_V(n - 5)
+            upper_clip_and_max(n, 3)
+            upper_clip_and_max(n, 2)
+            if n >= 5 and not scalar_divides(n - 5):
+                divide_and_store(n - 5, 0, GROUP, False)
 
-            if live(n - 1):
+            if n >= 1:
                 negate_max(n - 1)
-            if live(n - 5):
-                divide_S(n - 5)
-            if live(n - 1):
+            if n >= 5 and scalar_divides(n - 5):
+                divide_and_store(n - 5, 0, GROUP, True)
+            if n >= 1:
                 exp(n - 1, 1)
                 exp(n - 1, 0)
-            turning = n >= 2 and (n - 2) % GROUPS < 2 and live(n - n % GROUPS + GROUPS)
-            half = n - n % GROUPS + GROUPS + 2 * ((n - 2) % GROUPS)
+            turned_now = n - n % GROUPS + GROUPS + 2 * (n % GROUPS - 2)
+            turning = n % GROUPS >= 2 and turned_now < N
             if turning:
-                turn_queries(half, 2)
-            if live(n - 2):
+                turn_queries(turned_now, 2)
+            if n >= 2:
                 turn_e(n - 2, 3)
                 turn_e(n - 2, 2)
             if n == 0:
-                turn_x(0, 0)
-                copy_x(0, 0)
-            if live(n + 1):
+                turn_and_copy_x(0, 0)
+            if n + 1 < N:
                 score_matmul(n + 1, 0)
                 score_matmul(n + 1, 1)
             if n == 0:
-                turn_x(0, 1)
-                copy_x(0, 1)
-                turn_x(1, 0)
-                copy_x(1, 0)
+                turn_and_copy_x(0, 1)
+                turn_queries(2, 2)
+                copy_queries(2, 2)
             if n == 1:
-                for half_x in range(2):
-                    turn_x(2, half_x)
-                    copy_x(2, half_x)
-            if live(n - 2):
-                copy_e(n - 2, 1)
-                copy_e(n - 2, 0)
-            if live(n - 4):
-                weighted_sums(n - 4)
-            if live(n - 1):
+                turn_and_copy_x(2, 0)
+                turn_and_copy_x(2, 1)
+            if n >= 2:
+                copy_e(n - 2, 1, nc.scalar.copy)
+                copy_e(n - 2, 0, nc.scalar.copy)
+            if n == 3:
+                value_matmuls(0)
+                value_matmuls(1)
+            if n >= 4:
+                group_sums(n - 4)
+            if n >= 1:
                 turn_e(n - 1, 1)
                 turn_e(n - 1, 0)
                 exp(n - 1, 3)
                 exp(n - 1, 2)
             if n == 1:
-                for half_x in range(2):
-                    turn_x(3, half_x)
-                    copy_x(3, half_x)
+                turn_and_copy_x(3, 0)
+                turn_and_copy_x(3, 1)
             if turning:
-                copy_queries(half, 2)
-            if n == 3:
-                value_matmuls(0)
-                value_matmuls(1)
-                for j in range(HK):
-                    add_bias(j)
-                for j in range(HK):
-                    quantise_v(j)
-            if live(n + 1):
+                copy_queries(turned_now, 2)
+            if n + 1 < N:
                 score_matmul(n + 1, 2)
                 score_matmul(n + 1, 3)
             if n == 0:
-                turn_queries(2, 2)
-                copy_queries(2, 2)
-                turn_x(1, 1)
-                copy_x(1, 1)
+                turn_and_copy_x(1, 0)
+                turn_and_copy_x(1, 1)
 
         last = N - 1
+
+        def pair_sums(b):
+            sums = psum_scores.tile([P, PAIR, D], F32, tag="scores", name="pair_sums")
+            weighted_sums(last, b * PAIR, (b + 1) * PAIR, sums)
+
         lower_clip(last, 1, nc.vector)
         turn_e(last - 1, 3)
         turn_e(last - 1, 2)
@@ -487,33 +445,29 @@ def tile_multiqueryattention_pa_kernel(tc, x, Wv, bv, q, k, out):
         copy_e(last - 1, 1, nc.vector.tensor_copy)
         negate_max(last)
         invert_sums(last - 3)
-        quantise_e(last - 2)
-        weighted_sums(last - 3)
+        quantise_e(last - 2, 0, GROUP)
+        group_sums(last - 3)
         exp(last, 1)
         exp(last, 0)
         turn_e(last, 1)
         turn_e(last, 0)
-        divide_V(last - 4)
         exp(last, 3)
         exp(last, 2)
         turn_e(last, 3)
         turn_e(last, 2)
-        divide_S(last - 4)
-        quantise_e(last - 1)
-        weighted_sums(last - 2)
+        divide_and_store(last - 4, 0, GROUP, True)
+        quantise_e(last - 1, 0, GROUP)
+        group_sums(last - 2)
         copy_e(last, 0, nc.vector.tensor_copy)
-        quantise_pair(last, 0)
-        weighted_sums_pair(last, 0)
-        divide_V(last - 3)
-        divide_S(last - 3)
+        quantise_e(last, 0, PAIR)
+        pair_sums(0)
+        divide_and_store(last - 3, 0, GROUP, True)
         copy_e(last, 1, nc.vector.tensor_copy)
-        weighted_sums(last - 1)
+        group_sums(last - 1)
         invert_sums(last - 1)
-        quantise_pair(last, 1)
-        weighted_sums_pair(last, 1)
-        divide_S(last - 2)
-        divide_V(last - 2)
-        divide_pair(last, 0)
-        divide_S(last - 1)
-        divide_V(last - 1)
-        divide_pair(last, 1)
+        quantise_e(last, PAIR, GROUP)
+        pair_sums(1)
+        divide_and_store(last - 2, 0, GROUP, True)
+        divide_and_store(last, 0, PAIR, False)
+        divide_and_store(last - 1, 0, GROUP, True)
+        divide_and_store(last, PAIR, GROUP, False)

from contextlib import ExitStack
import math

import concourse.mybir as mybir
from concourse.masks import make_identity

F32 = mybir.dt.float32
BF16 = mybir.dt.bfloat16
U32 = mybir.dt.uint32
U8 = mybir.dt.uint8
FP8X4 = mybir.dt.float8_e4m3fn_x4
ALU = mybir.AluOpType
ACT = mybir.ActivationFunctionType

P = 128
PACK = 4
K_PASS = P * PACK

T = 512
C = 2048
H = 16
HK = 2
D = 128
ROW_TILES = T // P
PASSES = C // K_PASS
PAIR = 2
GROUP = 4
GROUPS = H // GROUP
N = ROW_TILES * GROUPS

SCALE = 1.0 / math.sqrt(D)
CLIP = 100.0
RAW_CLIP = CLIP / SCALE

FLOPS = 2 * T * C * HK * D + 2 * 2 * H * T * T * D


def tile_multiqueryattention_pa_kernel(tc, x, Wv, bv, q, k, out):
    nc = tc.nc
    with ExitStack() as ctx:
        ctx.enter_context(tc.manual_schedule())
        keep = ctx.enter_context(tc.tile_pool(name="keep", bufs=1))
        q_pool = ctx.enter_context(tc.tile_pool(name="q_pool", bufs=ROW_TILES))
        qT_pool = ctx.enter_context(tc.tile_pool(name="qT_pool", bufs=2))
        score_pool = ctx.enter_context(tc.tile_pool(name="score_pool", bufs=8))
        x_pool = ctx.enter_context(tc.tile_pool(name="x_pool", bufs=PASSES))
        e_pool = ctx.enter_context(tc.tile_pool(name="e_pool", bufs=6))
        code_pool = ctx.enter_context(tc.tile_pool(name="code_pool", bufs=5))
        out_pool = ctx.enter_context(tc.tile_pool(name="out_pool", bufs=8))
        stats = ctx.enter_context(tc.tile_pool(name="stats", bufs=16))
        psum_scores = ctx.enter_context(tc.psum_pool(name="psum_scores", bufs=GROUP))
        psum_turned = ctx.enter_context(tc.psum_pool(name="psum_turned", bufs=2))
        psum_sums = ctx.enter_context(tc.psum_pool(name="psum_sums", bufs=2))

        x_view = x.flatten_outer_dims().rearrange("(r i) c -> r i c", i=ROW_TILES)
        q_view = q.flatten_outer_dims().rearrange("(r i) c -> r i c", i=ROW_TILES)
        k_view = k.flatten_outer_dims().rearrange("(r i) c -> r i c", i=ROW_TILES)
        out_view = out.flatten_outer_dims().rearrange("(r i) c -> r i c", i=ROW_TILES)

        k_rows = keep.tile([P, ROW_TILES, HK * D], BF16)
        nc.sync.dma_start(out=k_rows[:], in_=k_view)
        q_rows = []
        for i in range(ROW_TILES):
            q_rows.append(q_pool.tile([P, H * D], BF16, name="q_rows"))

        def load_queries(i, first, end):
            cols = slice(first * GROUP * D, end * GROUP * D)
            nc.sync.dma_start(out=q_rows[i][:, cols], in_=q_view[:, i, cols])

        load_queries(0, 0, 1)
        load_queries(0, 1, GROUPS)
        x_rows = []
        for half in range(2):
            x_rows.append(keep.tile([P, ROW_TILES, C // 2], BF16, name="x_rows_%d" % half))
            nc.sync.dma_start(out=x_rows[half][:], in_=x_view[:, :, half * C // 2 : (half + 1) * C // 2])
        w_rows = keep.tile([P, C * HK * D // P], BF16)
        nc.sync.dma_start(
            out=w_rows[:].rearrange("p (s f) -> p s f", s=2 * PASSES),
            in_=Wv.rearrange("(s p e) c -> p s (e c)", p=P, e=2),
        )
        bias_rows = keep.tile([P, HK * D], BF16)
        nc.sync.dma_start(out=bias_rows[:], in_=bv.partition_broadcast(P))
        for i in range(1, ROW_TILES):
            load_queries(i, 0, GROUPS)

        warm_in = keep.tile([P, 1], F32)
        nc.vector.memset(warm_in[:], 0.0)
        warm_out = keep.tile([P, 1], F32)
        nc.scalar.activation(out=warm_out[:], in_=warm_in[:], func=ACT.Exp)
        ident_bf16 = keep.tile([P, P], BF16)
        make_identity(nc, ident_bf16[:])
        ident_f32 = keep.tile([P, P], F32)
        make_identity(nc, ident_f32[:])

        kT = [None] * HK
        k_turned = [None] * HK

        def turn_keys(j):
            k_turned[j] = psum_turned.tile([P, ROW_TILES, P], BF16, tag="turned", name="k_turned")
            for i in range(ROW_TILES):
                nc.tensor.transpose(k_turned[j][:, i, :], k_rows[:, i, j * D : (j + 1) * D], ident_bf16[:])

        def copy_keys(j, copy):
            kT[j] = keep.tile([P, T], BF16, name="kT_%d" % j)
            copy(
                out=kT[j][:].rearrange("p (u r e) -> p u r e", u=2, e=2),
                in_=k_turned[j][:].rearrange("p (u e) r -> p u r e", u=2),
            )

        qT = [None] * N
        q_turned = [None] * N

        def turn_queries(n, count):
            i, hq = divmod(n, GROUPS)
            q_turned[n] = psum_sums.tile([P, count * GROUP, P], BF16, tag="sums", name="q_turned")
            for a in range(count * GROUP):
                h = hq * GROUP + a
                nc.tensor.transpose(q_turned[n][:, a, :], q_rows[i][:, h * D : (h + 1) * D], ident_bf16[:])

        def copy_queries(n, count):
            turned = qT_pool.tile([P, count * GROUP, P], BF16, name="qT_%d" % (n % GROUPS))
            nc.scalar.copy(out=turned[:], in_=q_turned[n][:])
            for c in range(count):
                qT[n + c] = turned[:, c * GROUP : (c + 1) * GROUP, :]

        def turn_block(turned, b, block):
            words = block.bitcast(F32)
            for u in range(2):
                nc.tensor.transpose(turned[:, b, u, :], words[:, u * P : (u + 1) * P], ident_f32[:])

        def copy_turned(grouped, half, turned, copy):
            words = grouped[:].bitcast(F32).rearrange("p (b r u) -> p b r u", b=4, u=2)
            copy(
                out=words[:, 2 * half : 2 * half + 2, :, :],
                in_=turned[:].rearrange("p b u r -> p b r u"),
            )

        w_grouped = keep.tile([P, PASSES * HK * D * PACK], BF16, align_bytes=64)
        w_codes = keep.tile([P, PASSES, HK * D], U32, align_bytes=64)
        w_scales = keep.tile([P, PASSES, HK * D], U8, align_bytes=64)
        x_codes = keep.tile([P, PASSES, T], U32, align_bytes=64)
        x_scales = keep.tile([P, PASSES, T], U8, align_bytes=64)
        v_grouped = keep.tile([P, HK, D, PACK], BF16, align_bytes=64)
        v_codes = []
        v_scales = []
        for j in range(HK):
            v_codes.append(keep.tile([P, D], U32, align_bytes=64, name="v_codes_%d" % j))
            v_scales.append(keep.tile([P, D], U8, align_bytes=64, name="v_scales_%d" % j))
        x_grouped = [None] * PASSES
        v_sums = []

        def group_w(g):
            cols = slice(g * HK * D * PACK, (g + 1) * HK * D * PACK)
            nc.vector.tensor_copy(
                out=w_grouped[:, cols].rearrange("p (c t) -> p c t", t=PACK),
                in_=w_rows[:, cols].rearrange("p (t c) -> p c t", t=PACK),
            )

        def quantise_w():
            nc.vector.quantize_mx(
                out=w_codes[:].rearrange("p g c -> p (g c)").bitcast(FP8X4),
                scales=w_scales[:].rearrange("p g c -> p (g c)"),
                in_=w_grouped[:],
            )

        def turn_and_copy_x(g, half):
            if half == 0:
                x_grouped[g] = x_pool.tile([P, 4 * K_PASS], BF16, align_bytes=64, name="x_grouped")
            x_turned = psum_sums.tile([P, 2, 2, P], F32, tag="sums", name="x_turned")
            part, k0 = divmod(g * K_PASS, C // 2)
            for b in range(2):
                turn_block(x_turned, b, x_rows[part][:, 2 * half + b, k0 : k0 + K_PASS])
            copy_turned(x_grouped[g], half, x_turned, nc.scalar.copy)

        def quantise_x(g):
            nc.vector.quantize_mx(out=x_codes[:, g, :].bitcast(FP8X4), scales=x_scales[:, g, :], in_=x_grouped[g][:])

        def value_matmuls(j):
            v_sums.append(psum_sums.tile([P, ROW_TILES, D], F32, tag="sums", name="v_sums"))
            for i in range(ROW_TILES):
                for g in range(PASSES):
                    nc.tensor.matmul_mx(
                        out=v_sums[j][:, i, :],
                        lhsT=x_codes[:, g, i * P : (i + 1) * P].bitcast(FP8X4),
                        lhsT_scale=x_scales[:, g, i * P : (i + 1) * P],
                        rhs=w_codes[:, g, j * D : (j + 1) * D].bitcast(FP8X4),
                        rhs_scale=w_scales[:, g, j * D : (j + 1) * D],
                        start=(g == 0),
                        stop=(g == PASSES - 1),
                    )

        def add_bias(j):
            nc.vector.tensor_tensor(
                out=v_grouped[:, j, :, :],
                in0=v_sums[j][:].rearrange("p t c -> p c t"),
                in1=bias_rows[:, j * D : (j + 1) * D].unsqueeze(2).to_broadcast([P, D, PACK]),
                op=ALU.add,
            )

        def quantise_v(j):
            nc.vector.quantize_mx(
                out=v_codes[j][:].bitcast(FP8X4),
                scales=v_scales[j][:],
                in_=v_grouped[:, j, :, :].rearrange("p c t -> p (c t)"),
            )

        raw_scores = {}
        clipped = {}
        row_max = [None] * N
        neg_max = [None] * N
        row_sums = [None] * N
        inv_sums = [None] * N
        e_rows = {}
        e_turned = {}
        e_grouped = [None] * N
        e_codes = [None] * N
        e_scales = [None] * N
        o_sums = {}

        def kv_head(n):
            return (n % GROUPS) * GROUP * HK // H

        def score_matmul(n, a):
            raw_scores[n, a] = psum_scores.tile([P, T], F32, tag="scores", name="raw_scores")
            nc.tensor.matmul(
                out=raw_scores[n, a][:], lhsT=qT[n][:, a, :], rhs=kT[kv_head(n)][:], start=True, stop=True
            )

        def upper_clip_and_max(n, a):
            b, c = divmod(a, PAIR)
            if row_max[n] is None:
                row_max[n] = stats.tile([P, GROUP], F32, name="row_max")
            if (n, b) not in clipped:
                clipped[n, b] = score_pool.tile([P, PAIR, T], F32, name="clipped")
            nc.vector.tensor_scalar(
                out=clipped[n, b][:, c, :],
                in0=raw_scores[n, a][:],
                scalar1=RAW_CLIP,
                scalar2=-RAW_CLIP,
                op0=ALU.min,
                op1=ALU.max,
                accum_out=row_max[n][:, a : a + 1],
            )

        def lower_clip(n, b, engine):
            pair = clipped[n, b][:].rearrange("p a k -> p (a k)")
            engine.tensor_scalar(
                out=pair, in0=pair, scalar1=RAW_CLIP, scalar2=-RAW_CLIP, op0=ALU.min, op1=ALU.max
            )

        def negate_max(n):
            neg_max[n] = stats.tile([P, GROUP], F32, name="neg_max")
            nc.scalar.mul(out=neg_max[n][:], in_=row_max[n][:], mul=-SCALE)

        def sum_column(n, a):
            return (n % 2) * GROUP + a

        def exp(n, a):
            b, c = divmod(a, PAIR)
            if row_sums[n] is None:
                row_sums[n] = stats.tile([P, 2 * GROUP], F32, name="row_sums")
                row_sums[n + 1] = row_sums[n]
            if (n, b) not in e_rows:
                e_rows[n, b] = e_pool.tile([P, PAIR, T], BF16, name="e_rows")
            col = sum_column(n, a)
            nc.scalar.activation(
                out=e_rows[n, b][:, c, :],
                in_=clipped[n, b][:, c, :],
                func=ACT.Exp,
                bias=neg_max[n][:, a : a + 1],
                scale=SCALE,
                accum_out=row_sums[n][:, col : col + 1],
            )

        def turn_e(n, a):
            b, c = divmod(a, PAIR)
            if (n, b) not in e_turned:
                e_turned[n, b] = psum_turned.tile([P, PAIR, 2, P], F32, tag="turned", name="e_turned")
            turn_block(e_turned[n, b], c, e_rows[n, b][:, c, :])

        def copy_e(n, b, copy):
            if e_grouped[n] is None:
                e_grouped[n] = e_pool.tile([P, 4 * K_PASS], BF16, align_bytes=64, name="e_grouped")
            copy_turned(e_grouped[n], b, e_turned[n, b], copy)

        def quantise_e(n, first, end):
            if e_codes[n] is None:
                e_codes[n] = code_pool.tile([P, GROUP * P], U32, align_bytes=64, name="e_codes")
                e_scales[n] = code_pool.tile([P, GROUP * P], U8, align_bytes=64, name="e_scales")
            nc.vector.quantize_mx(
                out=e_codes[n][:, first * P : end * P].bitcast(FP8X4),
                scales=e_scales[n][:, first * P : end * P],
                in_=e_grouped[n][:, first * K_PASS : end * K_PASS],
            )

        def weighted_sums(n, first, end, sums):
            j = kv_head(n)
            o_sums[n, first] = sums
            for a in range(first, end):
                nc.tensor.matmul_mx(
                    out=sums[:, a - first, :],
                    lhsT=e_codes[n][:, a * P : (a + 1) * P].bitcast(FP8X4),
                    lhsT_scale=e_scales[n][:, a * P : (a + 1) * P],
                    rhs=v_codes[j][:].bitcast(FP8X4),
                    rhs_scale=v_scales[j][:],
                    start=True,
                    stop=True,
                )

        def group_sums(n):
            sums = psum_sums.tile([P, GROUP, D], F32, tag="sums", name="o_sums")
            weighted_sums(n, 0, GROUP, sums)

        def invert_sums(n):
            inv_sums[n] = stats.tile([P, 2 * GROUP], F32, name="inv_sums")
            inv_sums[n + 1] = inv_sums[n]
            nc.vector.reciprocal(out=inv_sums[n][:], in_=row_sums[n][:])

        def divide_and_store(n, first, end, on_scalar):
            i, hq = divmod(n, GROUPS)
            sums = o_sums[n, first]
            o_rows = out_pool.tile([P, end - first, D], F32, name="o_rows")
            col = sum_column(n, first)
            if on_scalar:
                for a in range(end - first):
                    nc.scalar.mul(
                        out=o_rows[:, a, :], in_=sums[:, a, :], mul=inv_sums[n][:, col + a : col + a + 1]
                    )
            else:
                nc.vector.tensor_tensor(
                    out=o_rows[:],
                    in0=sums[:],
                    in1=inv_sums[n][:, col : col + end - first].unsqueeze(2).to_broadcast([P, end - first, D]),
                    op=ALU.mult,
                )
            cols = slice((hq * GROUP + first) * D, (hq * GROUP + end) * D)
            nc.sync.dma_start(out=out_view[:, i, cols], in_=o_rows[:].rearrange("p a d -> p (a d)"))

        def scalar_divides(n):
            return n % 4 == 1

        turn_keys(0)
        copy_keys(0, nc.vector.tensor_copy)
        turn_queries(0, 1)
        copy_queries(0, 1)
        for a in range(GROUP):
            score_matmul(0, a)

        for n in range(N):
            upper_clip_and_max(n, 1 if n > 0 else 0)
            if n >= 3:
                quantise_e(n - 3, 0, GROUP)
            if n >= 4 and n % 2 == 0:
                invert_sums(n - 4)
            if n >= 1:
                lower_clip(n - 1, 1, nc.vector)
            if n == 2:
                quantise_x(0)
                quantise_x(1)
                for g in range(PASSES):
                    group_w(g)
            if n == 3:
                quantise_x(2)
                quantise_x(3)
            if n == 4:
                for j in range(HK):
                    add_bias(j)
                for j in range(HK):
                    quantise_v(j)
            upper_clip_and_max(n, 0 if n > 0 else 1)
            lower_clip(n, 0, nc.gpsimd)
            if n == 0:
                turn_queries(1, 1)
                copy_queries(1, 1)
                turn_keys(1)
                copy_keys(1, nc.scalar.copy)
            if n == 3:
                quantise_w()
            upper_clip_and_max(n, 3)
            upper_clip_and_max(n, 2)
            if n >= 5 and not scalar_divides(n - 5):
                divide_and_store(n - 5, 0, GROUP, False)

            if n >= 1:
                negate_max(n - 1)
            if n >= 5 and scalar_divides(n - 5):
                divide_and_store(n - 5, 0, GROUP, True)
            if n >= 1:
                exp(n - 1, 1)
                exp(n - 1, 0)
            turned_now = n - n % GROUPS + GROUPS + 2 * (n % GROUPS - 2)
            turning = n % GROUPS >= 2 and turned_now < N
            if turning:
                turn_queries(turned_now, 2)
            if n >= 2:
                turn_e(n - 2, 3)
                turn_e(n - 2, 2)
            if n == 0:
                turn_and_copy_x(0, 0)
            if n + 1 < N:
                score_matmul(n + 1, 0)
                score_matmul(n + 1, 1)
            if n == 0:
                turn_and_copy_x(0, 1)
                turn_queries(2, 2)
                copy_queries(2, 2)
            if n == 1:
                turn_and_copy_x(2, 0)
                turn_and_copy_x(2, 1)
            if n >= 2:
                copy_e(n - 2, 1, nc.scalar.copy)
                copy_e(n - 2, 0, nc.scalar.copy)
            if n == 3:
                value_matmuls(0)
                value_matmuls(1)
            if n >= 4:
                group_sums(n - 4)
            if n >= 1:
                turn_e(n - 1, 1)
                turn_e(n - 1, 0)
                exp(n - 1, 3)
                exp(n - 1, 2)
            if n == 1:
                turn_and_copy_x(3, 0)
                turn_and_copy_x(3, 1)
            if turning:
                copy_queries(turned_now, 2)
            if n + 1 < N:
                score_matmul(n + 1, 2)
                score_matmul(n + 1, 3)
            if n == 0:
                turn_and_copy_x(1, 0)
                turn_and_copy_x(1, 1)

        last = N - 1

        def pair_sums(b):
            sums = psum_scores.tile([P, PAIR, D], F32, tag="scores", name="pair_sums")
            weighted_sums(last, b * PAIR, (b + 1) * PAIR, sums)

        lower_clip(last, 1, nc.vector)
        turn_e(last - 1, 3)
        turn_e(last - 1, 2)
        copy_e(last - 1, 0, nc.vector.tensor_copy)
        copy_e(last - 1, 1, nc.vector.tensor_copy)
        negate_max(last)
        invert_sums(last - 3)
        quantise_e(last - 2, 0, GROUP)
        group_sums(last - 3)
        exp(last, 1)
        exp(last, 0)
        turn_e(last, 1)
        turn_e(last, 0)
        exp(last, 3)
        exp(last, 2)
        turn_e(last, 3)
        turn_e(last, 2)
        divide_and_store(last - 4, 0, GROUP, True)
        quantise_e(last - 1, 0, GROUP)
        group_sums(last - 2)
        copy_e(last, 0, nc.vector.tensor_copy)
        quantise_e(last, 0, PAIR)
        pair_sums(0)
        divide_and_store(last - 3, 0, GROUP, True)
        copy_e(last, 1, nc.vector.tensor_copy)
        group_sums(last - 1)
        invert_sums(last - 1)
        quantise_e(last, PAIR, GROUP)
        pair_sums(1)
        divide_and_store(last - 2, 0, GROUP, True)
        divide_and_store(last, 0, PAIR, False)
        divide_and_store(last - 1, 0, GROUP, True)
        divide_and_store(last, PAIR, GROUP, False)
